import numpy as np
import ml_dtypes


def mxq(x, axis, fmt="e4m3"):
    dtype, down = {"e4m3": (ml_dtypes.float8_e4m3fn, 7), "e5m2": (ml_dtypes.float8_e5m2, 14)}[fmt]
    v = np.moveaxis(np.asarray(x, np.float32).astype(ml_dtypes.bfloat16).astype(np.float64), axis, -1)
    blocks = v.reshape(v.shape[:-1] + (-1, 32))
    amax = np.abs(blocks).max(-1, keepdims=True)
    byte = np.maximum(np.where(amax > 0, np.frexp(amax)[1] - 1 + 127, 0) - down, 1)
    scale = np.exp2(byte - 127.0)
    codes = (blocks / scale).astype(np.float32).astype(dtype).astype(np.float64)
    return np.moveaxis((codes * scale).reshape(v.shape), -1, axis)


WIDE = False


def mx_kscale(k):
    if not WIDE:
        return np.ones(k)
    levels = np.array([10, -10, 5, -5, 0])
    if k % 512:
        return np.exp2(np.random.permutation(np.resize(levels, k // 32))).repeat(32)
    a = np.empty((k // 512, 16))
    for p in range(k // 512):
        a[p, :8] = np.random.permutation(np.resize(levels, 8))
        for g in range(8):
            far = levels[np.abs(levels - a[p, g]) >= 10]
            a[p, g + 8] = far[np.random.randint(len(far))]
    return np.exp2(a.ravel()).repeat(32)


BF16 = ml_dtypes.bfloat16


def bf(x):
    return np.asarray(x, np.float32).astype(BF16)


def f64(x):
    return np.asarray(x).astype(np.float64)


B, N, D_IN, D_H, NM = 4, 512, 256, 256, 5
F = D_IN + D_H


def sigmoid(v):
    return 1.0 / (1.0 + np.exp(-v))


def draw0():
    t = mx_kscale(NM * F)
    s = mx_kscale(N)
    blk = np.repeat(np.array([1.0, 0.7, 1.4, 0.7, 1.4]), F)
    return {"cat_g": bf(np.random.standard_normal((B, N, NM * F)) * blk * t),
            "gate_w": bf(np.random.standard_normal((NM * F, 2 * D_H)) / np.sqrt(NM * F) / t[:, None]),
            "gate_b": bf(1.0 + 0.5 * np.random.standard_normal(2 * D_H)),
            "x": bf(np.random.standard_normal((B, N, D_IN)) * s[None, :, None]),
            "h": bf(np.random.standard_normal((B, N, D_H)) * s[None, :, None]),
            "support0": bf(np.random.standard_normal((N, N)) * 0.7 / np.sqrt(N) / s[None, :]),
            "support1": bf(np.random.standard_normal((N, N)) * 0.7 / np.sqrt(N) / s[None, :])}


def core(cat_g, gate_w, gate_b, x, h, support0, support1):
    gates = (mxq(f64(cat_g), 2, "e4m3") @ mxq(f64(gate_w), 0, "e4m3")) + f64(gate_b)
    r, u = np.split(gates, 2, axis=-1)
    r = sigmoid(r)
    u = sigmoid(u)
    rh = r * f64(h)
    cand_in = np.concatenate([f64(x), rh], axis=-1)
    cq = mxq(cand_in, 1, "e4m3")
    d1_s0 = mxq(f64(support0), 1, "e4m3") @ cq
    d1_s1 = mxq(f64(support1), 1, "e4m3") @ cq
    return rh, u, d1_s0, d1_s1


def e4m3fn_bytes(y):
    return np.clip(np.asarray(y, np.float64), -448.0, 448.0).astype(np.float32).astype(ml_dtypes.float8_e4m3fn).view(np.uint8)


def e4m3fn_values(b):
    return np.asarray(b, np.uint8).view(ml_dtypes.float8_e4m3fn).astype(np.float64)


def setup_inputs():
    d = draw0()
    x0 = np.asarray(d['cat_g']).astype(np.float64)
    s = (np.max(np.abs(x0), axis=(0, 1), keepdims=True) / 448.0).astype(np.float32)
    out = {}
    for k, v in d.items():
        if k == 'cat_g':
            out['cat_g_bytes'] = e4m3fn_bytes(x0 / s.astype(np.float64))
            out['cat_g_scale'] = s
        else:
            out[k] = v
    return out


def reference(cat_g_bytes, cat_g_scale, gate_w, gate_b, x, h, support0, support1):
    return core(e4m3fn_values(cat_g_bytes) * cat_g_scale.astype(np.float64), gate_w, gate_b, x, h, support0, support1)

@@ -1,0 +1,409 @@
+from contextlib import ExitStack
+
+import concourse.mybir as mybir
+from concourse.masks import make_identity
+
+F32 = mybir.dt.float32
+BF16 = mybir.dt.bfloat16
+U32 = mybir.dt.uint32
+U8 = mybir.dt.uint8
+FP8 = mybir.dt.float8_e4m3fn
+FP8X4 = mybir.dt.float8_e4m3fn_x4
+MULT = mybir.AluOpType.mult
+ADD = mybir.AluOpType.add
+SIGMOID = mybir.ActivationFunctionType.Sigmoid
+
+B, N, F, D = 4, 512, 2560, 256
+G = F // 512
+NG = 2 * D
+FLOPS = 2 * B * N * F * NG + 2 * 2 * B * N * N * 2 * D
+
+LOADS0 = ((0, 512), (512, 1536), (1536, 2560))
+PAD = 64
+
+
+def tile_dcgrucell_pb_kernel(
+    tc, cat_b, cat_s, gate_w, gate_b, x, h, support0, support1, out_0, out_1, out_2, out_3
+):
+    nc = tc.nc
+    outs_d = (out_2, out_3)
+
+    with ExitStack() as ctx:
+        keep = ctx.enter_context(tc.tile_pool(name="keep", bufs=1))
+        pool = ctx.enter_context(tc.tile_pool(name="pool", bufs=2))
+        psum = ctx.enter_context(tc.psum_pool(name="psum", bufs=4))
+        ctx.enter_context(tc.manual_schedule())
+
+        scale = keep.tile([128, G, 4], F32, name="scale")
+        nc.sync.dma_start(out=scale[:], in_=cat_s.rearrange("a b (g p t) -> p (a b g) t", p=128, t=4))
+
+        w_raw = {}
+        raw = {}
+
+        def load_w(g):
+            w_raw[g] = pool.tile([128, 4, NG], BF16, name="w_raw", bufs=3)
+            nc.sync.dma_start(out=w_raw[g][:], in_=gate_w[512 * g : 512 * (g + 1), :].rearrange("(p j) n -> p j n", j=4))
+
+        def load_cat0(c):
+            k0, k1 = LOADS0[c]
+            t_ = keep.tile([128, 4, k1 - k0 + PAD], U8, name="raw0_%d" % c, align_bytes=64)
+            nc.sync.dma_start(out=t_[:, :, 0 : k1 - k0], in_=cat_b[0].rearrange("(p t) k -> p t k", t=4)[:, :, k0:k1])
+            raw[(0, c)] = t_
+
+        def load_cat(b, hh):
+            t_ = pool.tile([128, 2, F + PAD], U8, name="raw", bufs=4, align_bytes=64)
+            nc.sync.dma_start(
+                out=t_[:, :, 0:F], in_=cat_b[b].rearrange("(p t) k -> p t k", t=4)[:, 2 * hh : 2 * hh + 2, :]
+            )
+            raw[(b, hh)] = t_
+
+        load_w(0)
+        load_cat0(0)
+        load_w(1)
+        load_cat0(1)
+        load_cat0(2)
+        load_w(2)
+        bias = keep.tile([128, NG], BF16, name="bias")
+
+        ident = keep.tile([128, 128], F32, name="ident")
+        make_identity(nc, ident[:])
+        warm = keep.tile([128, 1], F32, name="warm")
+        warm_out = keep.tile([128, 1], F32, name="warm_out")
+        nc.vector.memset(warm[:], 0.0)
+        nc.scalar.activation(out=warm_out[:], in_=warm[:], func=SIGMOID)
+
+        def ilv_views(dst, src):
+            return (
+                dst.rearrange("p (c i) t -> p c t i", i=4),
+                src.rearrange("p t (c i) -> p c t i", i=4),
+            )
+
+        def interleave(eng, dst, src):
+            d_, s_ = ilv_views(dst, src)
+            if eng == "V":
+                nc.vector.tensor_copy(out=d_, in_=s_)
+            if eng == "S":
+                nc.scalar.copy(out=d_, in_=s_)
+            if eng == "G":
+                nc.gpsimd.tensor_scalar(out=d_, in0=s_, scalar1=1.0, scalar2=0.0, op0=MULT, op1=ADD)
+
+        def quantize(codes, scales, grouped):
+            nc.vector.quantize_mx(
+                out=codes.bitcast(FP8X4), scales=scales, in_=grouped.rearrange("p c t -> p (c t)")
+            )
+
+        w_grp = {}
+        w_codes = {}
+        w_sc = {}
+
+        def w_ilv(g, eng, parts=1):
+            w_grp[g] = pool.tile([128, NG, 4], BF16, name="w_grp", bufs=2, align_bytes=64)
+            step = NG // parts
+            for c in range(0, NG, step):
+                interleave(eng, w_grp[g][:, c : c + step, :], w_raw[g][:, :, c : c + step])
+
+        def w_q(g):
+            w_codes[g] = keep.tile([128, NG], U32, name="w_codes%d" % g, align_bytes=64)
+            w_sc[g] = keep.tile([128, NG], U8, name="w_sc%d" % g, align_bytes=64)
+            quantize(w_codes[g][:], w_sc[g][:], w_grp[g][:])
+
+        wide = {}
+
+        def widen0(c):
+            k0, k1 = LOADS0[c]
+            for t in range(4):
+                if c == 0:
+                    wide[(0, t)] = pool.tile([128, F], BF16, name="wide", bufs=8, align_bytes=64)
+                nc.scalar.copy(out=wide[(0, t)][:, k0:k1], in_=raw[(0, c)][:, t, 0 : k1 - k0].bitcast(FP8))
+
+        def widen(b, t):
+            wide[(b, t)] = pool.tile([128, F], BF16, name="wide", bufs=8, align_bytes=64)
+            nc.scalar.copy(out=wide[(b, t)][:], in_=raw[(b, t // 2)][:, t % 2, 0:F].bitcast(FP8))
+
+        tr = {}
+
+        def transposes(i):
+            b, g = divmod(i, G)
+            for hh in range(2):
+                bank = psum.tile([128, 512], F32, name="tr")
+                tr[(i, hh)] = bank
+                for tt in range(2):
+                    words = wide[(b, 2 * hh + tt)][:].bitcast(F32)
+                    for u in range(2):
+                        c = 256 * u + 128 * tt
+                        nc.tensor.transpose(
+                            bank[:, c : c + 128], words[:, 256 * g + u : 256 * (g + 1) : 2], ident[:]
+                        )
+
+        grp = {}
+
+        def scale_evac(i, hh):
+            g = i % G
+            if hh == 0:
+                grp[i] = pool.tile([128, 512, 4], BF16, name="grp", bufs=3, align_bytes=64)
+            src = tr[(i, hh)][:].rearrange("p (u r) -> p u r", u=2).bitcast(BF16).rearrange("p u (r e) -> p r u e", e=2)
+            dst = grp[i][:, 256 * hh : 256 * (hh + 1), :].rearrange("p r (u e) -> p r u e", u=2)
+            sc = scale[:, g, :].rearrange("p (u e) -> p u e", u=2).unsqueeze(1).to_broadcast([128, 256, 2, 2])
+            nc.vector.tensor_tensor(out=dst, in0=src, in1=sc, op=MULT)
+
+        codes = {}
+        scb = {}
+
+        def q_cat(i):
+            codes[i] = pool.tile([128, 512], U32, name="codes", bufs=3, align_bytes=64)
+            scb[i] = pool.tile([128, 512], U8, name="scb", bufs=3, align_bytes=64)
+            quantize(codes[i][:], scb[i][:], grp[i][:])
+
+        gate = {}
+
+        def gates(i):
+            b, g = divmod(i, G)
+            for t in range(4):
+                if g == 0:
+                    gate[(b, t)] = psum.tile([128, NG], F32, name="gate")
+                c = slice(128 * t, 128 * (t + 1))
+                nc.tensor.matmul_mx(
+                    out=gate[(b, t)][:],
+                    lhsT=codes[i][:, c].bitcast(FP8X4),
+                    lhsT_scale=scb[i][:, c],
+                    rhs=w_codes[g][:].bitcast(FP8X4),
+                    rhs_scale=w_sc[g][:],
+                    start=(g == 0),
+                    stop=(g == G - 1),
+                )
+
+        sig = {}
+        gsum = {}
+
+        def bias_add(b, t, c0=0, c1=NG):
+            if (b, t) not in gsum:
+                gsum[(b, t)] = pool.tile([128, NG], F32, name="gsum", bufs=4)
+            nc.vector.tensor_tensor(
+                out=gsum[(b, t)][:, c0:c1], in0=gate[(b, t)][:, c0:c1], in1=bias[:, c0:c1], op=ADD
+            )
+
+        def sigm(b, t, c0=0, c1=NG):
+            if b not in sig:
+                sig[b] = pool.tile([128, 4, NG], F32, name="sig", bufs=2)
+            nc.scalar.activation(out=sig[b][:, t, c0:c1], in_=gsum[(b, t)][:, c0:c1], func=SIGMOID)
+
+        def store_u(b):
+            nc.sync.dma_start(out=out_1[b].rearrange("(p t) c -> p t c", t=4), in_=sig[b][:, :, D:NG])
+
+        x_t = {}
+        h_t = {}
+        cg = {}
+
+        def load_xh(b):
+            x_t[b] = keep.tile([128, 4, D], BF16, name="x%d" % b)
+            h_t[b] = keep.tile([128, 4, D], BF16, name="h%d" % b)
+            nc.sync.dma_start(out=x_t[b][:], in_=x[b].rearrange("(p t) c -> p t c", t=4))
+            nc.sync.dma_start(out=h_t[b][:], in_=h[b].rearrange("(p t) c -> p t c", t=4))
+
+        def x_ilv(b, eng):
+            cg[b] = pool.tile([128, 2 * D, 4], BF16, name="cg", bufs=3, align_bytes=64)
+            interleave(eng, cg[b][:, 0:D, :], x_t[b][:])
+
+        rh = {}
+
+        def rh_mul(b, t, eng):
+            if b not in rh:
+                rh[b] = pool.tile([128, 4, D], F32, name="rh", bufs=2)
+            e = nc.gpsimd if eng == "G" else nc.vector
+            e.tensor_tensor(out=rh[b][:, t, :], in0=sig[b][:, t, 0:D], in1=h_t[b][:, t, :], op=MULT)
+
+        def store_rh(b):
+            nc.sync.dma_start(out=out_0[b].rearrange("(p t) c -> p t c", t=4), in_=rh[b][:])
+
+        def rh_ilv(b, eng):
+            interleave(eng, cg[b][:, D : 2 * D, :], rh[b][:])
+
+        cc = {}
+        cs = {}
+
+        def q_cand(b, c0=0, c1=2 * D):
+            if b not in cc:
+                cc[b] = pool.tile([128, 2 * D], U32, name="cc", bufs=3, align_bytes=64)
+                cs[b] = pool.tile([128, 2 * D], U8, name="cs", bufs=3, align_bytes=64)
+            quantize(cc[b][:, c0:c1], cs[b][:, c0:c1], cg[b][:, c0:c1, :])
+
+        sup_raw = {}
+        sup_grp = {}
+        sup_codes = {}
+        sup_sc = {}
+
+        def load_sup(s):
+            sup_raw[s] = keep.tile([128, 4, N], BF16, name="sup_raw%d" % s)
+            nc.sync.dma_start(out=sup_raw[s][:], in_=(support0, support1)[s].rearrange("(p t) k -> p t k", t=4))
+
+        def sup_unit(s, hh):
+            if hh == 0:
+                sup_grp[s] = pool.tile([128, N, 4], BF16, name="w_grp", bufs=2, align_bytes=64)
+            bank = psum.tile([128, 512], F32, name="tr")
+            for tt in range(2):
+                words = sup_raw[s][:, 2 * hh + tt, :].bitcast(F32)
+                for u in range(2):
+                    c = 256 * u + 128 * tt
+                    nc.tensor.transpose(bank[:, c : c + 128], words[:, u:256:2], ident[:])
+            dst = sup_grp[s][:, 256 * hh : 256 * (hh + 1), :].rearrange("p r t -> p (r t)").bitcast(F32)
+            nc.scalar.copy(
+                out=dst.rearrange("p (r u) -> p r u", u=2), in_=bank[:].rearrange("p (u r) -> p r u", u=2)
+            )
+
+        def q_sup(s):
+            sup_codes[s] = keep.tile([128, N], U32, name="sup_codes%d" % s, align_bytes=64)
+            sup_sc[s] = keep.tile([128, N], U8, name="sup_sc%d" % s, align_bytes=64)
+            quantize(sup_codes[s][:], sup_sc[s][:], sup_grp[s][:])
+
+        dt = {}
+
+        def d1_tile(b, s):
+            if (b, s) not in dt:
+                dt[(b, s)] = pool.tile([128, 4, 2 * D], F32, name="dt", bufs=3)
+            return dt[(b, s)]
+
+        def d1_mm(out, b, s, t, c0, c1):
+            c = slice(128 * t, 128 * (t + 1))
+            nc.tensor.matmul_mx(
+                out=out,
+                lhsT=sup_codes[s][:, c].bitcast(FP8X4),
+                lhsT_scale=sup_sc[s][:, c],
+                rhs=cc[b][:, c0:c1].bitcast(FP8X4),
+                rhs_scale=cs[b][:, c0:c1],
+                start=True,
+                stop=True,
+            )
+
+        def store_d1(b, s, c0=0, c1=2 * D, t0=0, t1=4):
+            nc.sync.dma_start(
+                out=outs_d[s][b].rearrange("(p t) c -> p t c", t=4)[:, t0:t1, c0:c1], in_=dt[(b, s)][:, t0:t1, c0:c1]
+            )
+
+        def d1_full(b, j):
+            s, t = divmod(j, 4)
+            dtile = d1_tile(b, s)
+            bank = psum.tile([128, 512], F32, name="tr")
+            d1_mm(bank[:], b, s, t, 0, 2 * D)
+            nc.scalar.copy(out=dtile[:, t, :], in_=bank[:])
+            if t == 3:
+                store_d1(b, s)
+
+        def d1_half(b, j, c0, eng):
+            s, tp = divmod(j, 2)
+            dtile = d1_tile(b, s)
+            bank = psum.tile([128, 512], F32, name="tr")
+            for q in range(2):
+                d1_mm(bank[:, D * q : D * (q + 1)], b, s, 2 * tp + q, c0, c0 + D)
+            dst = dtile[:, 2 * tp : 2 * tp + 2, c0 : c0 + D]
+            src = bank[:].rearrange("p (q c) -> p q c", q=2)
+            if eng == "S":
+                nc.scalar.copy(out=dst, in_=src)
+            if eng == "V":
+                nc.vector.tensor_copy(out=dst, in_=src)
+
+        w_ilv(0, "V")
+        widen0(0)
+        transposes(0)
+        w_q(0)
+        widen0(1)
+        w_ilv(1, "V")
+        widen0(2)
+        load_w(3)
+        w_ilv(2, "G", 4)
+        load_w(4)
+        nc.sync.dma_start(out=bias[:], in_=gate_b.partition_broadcast(128))
+        load_cat(1, 0)
+        load_cat(1, 1)
+        load_sup(0)
+        load_sup(1)
+        load_xh(0)
+        load_cat(2, 0)
+        load_cat(2, 1)
+        load_xh(1)
+        load_xh(2)
+        load_xh(3)
+
+        NS = B * G
+        D1_AT = {}
+        for b in range(3):
+            for j in range(8):
+                D1_AT.setdefault(5 * b + 8 + (j // 2 if b < 2 else j // 4), []).append((b, j))
+
+        for i in range(NS):
+            b, g = divmod(i, G)
+            if b < 3 and g < 4:
+                widen(b + 1, g)
+            if b >= 1 and g == 1:
+                bias_add(b - 1, 0)
+                bias_add(b - 1, 1)
+            scale_evac(i, 0)
+            if i > 0:
+                q_cat(i - 1)
+            if i == 0:
+                w_q(1)
+            if i == 1:
+                w_q(2)
+                w_ilv(3, "S")
+                w_ilv(4, "G", 4)
+            if i == 2:
+                w_q(3)
+                sup_unit(0, 0)
+                sup_unit(0, 1)
+            if i == 2:
+                load_cat(3, 0)
+            if i == 3:
+                w_q(4)
+                q_sup(0)
+                sup_unit(1, 0)
+                sup_unit(1, 1)
+            if i == 4:
+                load_cat(3, 1)
+                q_sup(1)
+                x_ilv(0, "S")
+            if b >= 1 and g == 1:
+                bias_add(b - 1, 2)
+                bias_add(b - 1, 3)
+                for t in range(4):
+                    sigm(b - 1, t)
+                    rh_mul(b - 1, t, "G")
+                store_u(b - 1)
+                store_rh(b - 1)
+            scale_evac(i, 1)
+            if b >= 1 and g == 2:
+                rh_ilv(b - 1, "S")
+                if b < 3:
+                    x_ilv(b, "S")
+            if b >= 1 and g == 3:
+                q_cand(b - 1)
+            if i == 14:
+                x_ilv(3, "S")
+            if i == 15:
+                q_cand(3, 0, D)
+            if i + 1 < NS:
+                transposes(i + 1)
+            if i > 0:
+                gates(i - 1)
+            for bb, j in D1_AT.get(i, ()):
+                d1_full(bb, j)
+            if i == 17:
+                for j in range(4):
+                    d1_half(3, j, 0, "S")
+
+        q_cat(NS - 1)
+        gates(NS - 1)
+        for t in range(4):
+            bias_add(3, t, 0, D)
+            sigm(3, t, 0, D)
+        for t in range(4):
+            rh_mul(3, t, "V")
+        store_rh(3)
+        rh_ilv(3, "V")
+        q_cand(3, D, 2 * D)
+        for t in range(4):
+            bias_add(3, t, D, NG)
+            sigm(3, t, D, NG)
+        store_u(3)
+        for j in range(4):
+            d1_half(3, j, D, "V" if j % 2 else "S")
+            if j % 2:
+                store_d1(3, j // 2)

@@ -10,12 +10,12 @@ U8 = mybir.dt.uint8
 FP8 = mybir.dt.float8_e4m3fn
 FP8X4 = mybir.dt.float8_e4m3fn_x4
 MULT = mybir.AluOpType.mult
-ADD = mybir.AluOpType.add
 SIGMOID = mybir.ActivationFunctionType.Sigmoid
 
 B, N, F, D = 4, 512, 2560, 256
 G = F // 512
 NG = 2 * D
+NS = B * G
 FLOPS = 2 * B * N * F * NG + 2 * 2 * B * N * N * 2 * D
 
 LOADS0 = ((0, 512), (512, 1536), (1536, 2560))
@@ -32,10 +32,15 @@ def tile_dcgrucell_pb_kernel(
         keep = ctx.enter_context(tc.tile_pool(name="keep", bufs=1))
         pool = ctx.enter_context(tc.tile_pool(name="pool", bufs=2))
         psum = ctx.enter_context(tc.psum_pool(name="psum", bufs=4))
-        ctx.enter_context(tc.manual_schedule())
 
-        scale = keep.tile([128, G, 4], F32, name="scale")
-        nc.sync.dma_start(out=scale[:], in_=cat_s.rearrange("a b (g p t) -> p (a b g) t", p=128, t=4))
+        scale = {}
+
+        def load_scale(c):
+            k0, k1 = LOADS0[c]
+            scale[c] = keep.tile([128, k1 - k0], F32, name="scale%d" % c)
+            nc.sync.dma_start(
+                out=scale[c][:], in_=cat_s.rearrange("a b k -> (a b k)")[k0:k1].partition_broadcast(128)
+            )
 
         w_raw = {}
         raw = {}
@@ -57,35 +62,47 @@ def tile_dcgrucell_pb_kernel(
             )
             raw[(b, hh)] = t_
 
-        load_w(0)
+        x_t = {}
+        h_t = {}
+
+        def load_xh(b):
+            x_t[b] = keep.tile([128, 4, D], BF16, name="x%d" % b)
+            h_t[b] = keep.tile([128, 4, D], BF16, name="h%d" % b)
+            nc.sync.dma_start(out=x_t[b][:], in_=x[b].rearrange("(p t) c -> p t c", t=4))
+            nc.sync.dma_start(out=h_t[b][:], in_=h[b].rearrange("(p t) c -> p t c", t=4))
+
+        sup_raw = {}
+
+        def load_sup(s):
+            sup_raw[s] = keep.tile([128, 4, N], BF16, name="sup_raw%d" % s)
+            nc.sync.dma_start(out=sup_raw[s][:], in_=(support0, support1)[s].rearrange("(p t) k -> p t k", t=4))
+
+        load_scale(0)
         load_cat0(0)
-        load_w(1)
+        load_w(0)
+        load_scale(1)
         load_cat0(1)
+        load_w(1)
+        load_scale(2)
         load_cat0(2)
         load_w(2)
-        bias = keep.tile([128, NG], BF16, name="bias")
 
         ident = keep.tile([128, 128], F32, name="ident")
         make_identity(nc, ident[:])
+        brow = keep.tile([128, 128], BF16, name="brow")
+        nc.gpsimd.memset(brow[:], 0.0)
         warm = keep.tile([128, 1], F32, name="warm")
         warm_out = keep.tile([128, 1], F32, name="warm_out")
         nc.vector.memset(warm[:], 0.0)
         nc.scalar.activation(out=warm_out[:], in_=warm[:], func=SIGMOID)
 
-        def ilv_views(dst, src):
-            return (
-                dst.rearrange("p (c i) t -> p c t i", i=4),
-                src.rearrange("p t (c i) -> p c t i", i=4),
-            )
-
         def interleave(eng, dst, src):
-            d_, s_ = ilv_views(dst, src)
+            d_ = dst.rearrange("p (c i) t -> p c t i", i=4)
+            s_ = src.rearrange("p t (c i) -> p c t i", i=4)
             if eng == "V":
                 nc.vector.tensor_copy(out=d_, in_=s_)
             if eng == "S":
                 nc.scalar.copy(out=d_, in_=s_)
-            if eng == "G":
-                nc.gpsimd.tensor_scalar(out=d_, in0=s_, scalar1=1.0, scalar2=0.0, op0=MULT, op1=ADD)
 
         def quantize(codes, scales, grouped):
             nc.vector.quantize_mx(
@@ -96,11 +113,9 @@ def tile_dcgrucell_pb_kernel(
         w_codes = {}
         w_sc = {}
 
-        def w_ilv(g, eng, parts=1):
-            w_grp[g] = pool.tile([128, NG, 4], BF16, name="w_grp", bufs=2, align_bytes=64)
-            step = NG // parts
-            for c in range(0, NG, step):
-                interleave(eng, w_grp[g][:, c : c + step, :], w_raw[g][:, :, c : c + step])
+        def w_ilv(g, eng):
+            w_grp[g] = pool.tile([128, NG, 4], BF16, name="w_grp", bufs=3, align_bytes=64)
+            interleave(eng, w_grp[g][:], w_raw[g][:])
 
         def w_q(g):
             w_codes[g] = keep.tile([128, NG], U32, name="w_codes%d" % g, align_bytes=64)
@@ -109,42 +124,47 @@ def tile_dcgrucell_pb_kernel(
 
         wide = {}
 
-        def widen0(c):
-            k0, k1 = LOADS0[c]
-            for t in range(4):
-                if c == 0:
-                    wide[(0, t)] = pool.tile([128, F], BF16, name="wide", bufs=8, align_bytes=64)
-                nc.scalar.copy(out=wide[(0, t)][:, k0:k1], in_=raw[(0, c)][:, t, 0 : k1 - k0].bitcast(FP8))
-
-        def widen(b, t):
-            wide[(b, t)] = pool.tile([128, F], BF16, name="wide", bufs=8, align_bytes=64)
-            nc.scalar.copy(out=wide[(b, t)][:], in_=raw[(b, t // 2)][:, t % 2, 0:F].bitcast(FP8))
-
-        tr = {}
-
-        def transposes(i):
+        def scaled(i, t):
             b, g = divmod(i, G)
-            for hh in range(2):
-                bank = psum.tile([128, 512], F32, name="tr")
-                tr[(i, hh)] = bank
-                for tt in range(2):
-                    words = wide[(b, 2 * hh + tt)][:].bitcast(F32)
-                    for u in range(2):
-                        c = 256 * u + 128 * tt
-                        nc.tensor.transpose(
-                            bank[:, c : c + 128], words[:, 256 * g + u : 256 * (g + 1) : 2], ident[:]
-                        )
+            wide[(i, t)] = pool.tile([128, 512], BF16, name="wide", bufs=16)
+            c = (g + 1) // 2
+            k0 = 512 * g - LOADS0[c][0]
+            if b == 0:
+                src = raw[(0, c)][:, t, k0 : k0 + 512]
+            else:
+                src = raw[(b, t // 2)][:, t % 2, 512 * g : 512 * (g + 1)]
+            nc.vector.tensor_tensor(
+                out=wide[(i, t)][:], in0=src.bitcast(FP8), in1=scale[c][:, k0 : k0 + 512], op=MULT
+            )
+
+        def copy_out(eng, out, in_):
+            if eng == "V":
+                nc.vector.tensor_copy(out=out, in_=in_)
+            if eng == "S":
+                nc.scalar.copy(out=out, in_=in_)
+
+        def turn(words, grouped, eng):
+            bank = psum.tile([128, 512], F32, name="tr")
+            for tt in range(2):
+                for u in range(2):
+                    c = 256 * u + 128 * tt
+                    nc.tensor.transpose(bank[:, c : c + 128], words[tt][:, u:256:2], ident[:])
+            copy_out(
+                eng,
+                grouped.rearrange("p r t -> p (r t)").bitcast(F32).rearrange("p (r u) -> p r u", u=2),
+                bank[:].rearrange("p (u r) -> p r u", u=2),
+            )
 
         grp = {}
 
-        def scale_evac(i, hh):
-            g = i % G
-            if hh == 0:
+        def turn_cat(i, hh, eng):
+            if i not in grp:
                 grp[i] = pool.tile([128, 512, 4], BF16, name="grp", bufs=3, align_bytes=64)
-            src = tr[(i, hh)][:].rearrange("p (u r) -> p u r", u=2).bitcast(BF16).rearrange("p u (r e) -> p r u e", e=2)
-            dst = grp[i][:, 256 * hh : 256 * (hh + 1), :].rearrange("p r (u e) -> p r u e", u=2)
-            sc = scale[:, g, :].rearrange("p (u e) -> p u e", u=2).unsqueeze(1).to_broadcast([128, 256, 2, 2])
-            nc.vector.tensor_tensor(out=dst, in0=src, in1=sc, op=MULT)
+            turn(
+                [wide[(i, 2 * hh + tt)][:].bitcast(F32) for tt in range(2)],
+                grp[i][:, 256 * hh : 256 * (hh + 1), :],
+                eng,
+            )
 
         codes = {}
         scb = {}
@@ -158,62 +178,71 @@ def tile_dcgrucell_pb_kernel(
 
         def gates(i):
             b, g = divmod(i, G)
-            for t in range(4):
+            for m in range(4):
                 if g == 0:
-                    gate[(b, t)] = psum.tile([128, NG], F32, name="gate")
-                c = slice(128 * t, 128 * (t + 1))
+                    gate[(b, m)] = psum.tile([128, N], F32, name="gate")
+                c = slice(128 * m, 128 * (m + 1))
                 nc.tensor.matmul_mx(
-                    out=gate[(b, t)][:],
-                    lhsT=codes[i][:, c].bitcast(FP8X4),
-                    lhsT_scale=scb[i][:, c],
-                    rhs=w_codes[g][:].bitcast(FP8X4),
-                    rhs_scale=w_sc[g][:],
+                    out=gate[(b, m)][:],
+                    lhsT=w_codes[g][:, c].bitcast(FP8X4),
+                    lhsT_scale=w_sc[g][:, c],
+                    rhs=codes[i][:].bitcast(FP8X4),
+                    rhs_scale=scb[i][:],
                     start=(g == 0),
                     stop=(g == G - 1),
                 )
 
-        sig = {}
-        gsum = {}
+        bcol = keep.tile([128, 4], F32, name="bcol")
 
-        def bias_add(b, t, c0=0, c1=NG):
-            if (b, t) not in gsum:
-                gsum[(b, t)] = pool.tile([128, NG], F32, name="gsum", bufs=4)
-            nc.vector.tensor_tensor(
-                out=gsum[(b, t)][:, c0:c1], in0=gate[(b, t)][:, c0:c1], in1=bias[:, c0:c1], op=ADD
+        def bias_cols():
+            bf = keep.tile([128, 128], F32, name="bf")
+            nc.vector.tensor_copy(out=bf[:], in_=brow[:])
+            bank = psum.tile([128, 512], F32, name="tr")
+            nc.tensor.transpose(bank[:, 0:128], bf[:], ident[:])
+            nc.vector.tensor_copy(out=bcol[:], in_=bank[:, 0:4])
+
+        sig = {}
+
+        def sigm(b, m):
+            sig[(b, m)] = pool.tile([128, N], F32, name="sig", bufs=6)
+            nc.scalar.activation(
+                out=sig[(b, m)][:], in_=gate[(b, m)][:], func=SIGMOID, bias=bcol[:, m : m + 1]
             )
 
-        def sigm(b, t, c0=0, c1=NG):
-            if b not in sig:
-                sig[b] = pool.tile([128, 4, NG], F32, name="sig", bufs=2)
-            nc.scalar.activation(out=sig[b][:, t, c0:c1], in_=gsum[(b, t)][:, c0:c1], func=SIGMOID)
+        def sig_turn(b, half, tp):
+            bank = psum.tile([128, 512], F32, name="tr")
+            for tt in range(2):
+                for mm in range(2):
+                    c = 256 * tt + 128 * mm
+                    n0 = 128 * (2 * tp + tt)
+                    nc.tensor.transpose(bank[:, c : c + 128], sig[(b, 2 * half + mm)][:, n0 : n0 + 128], ident[:])
+            return bank[:].rearrange("p (t c) -> p t c", t=2)
+
+        rh = {}
+        ut = {}
+
+        def rh_part(b, tp):
+            if b not in rh:
+                rh[b] = pool.tile([128, 4, D], F32, name="rh", bufs=2)
+            t2 = slice(2 * tp, 2 * tp + 2)
+            nc.vector.tensor_tensor(out=rh[b][:, t2, :], in0=sig_turn(b, 0, tp), in1=h_t[b][:, t2, :], op=MULT)
+
+        def u_part(b, tp, eng="S"):
+            if b not in ut:
+                ut[b] = pool.tile([128, 4, D], F32, name="ut", bufs=2)
+            copy_out(eng, ut[b][:, 2 * tp : 2 * tp + 2, :], sig_turn(b, 1, tp))
+
+        def store_rh(b):
+            nc.sync.dma_start(out=out_0[b].rearrange("(p t) c -> p t c", t=4), in_=rh[b][:])
 
         def store_u(b):
-            nc.sync.dma_start(out=out_1[b].rearrange("(p t) c -> p t c", t=4), in_=sig[b][:, :, D:NG])
+            nc.sync.dma_start(out=out_1[b].rearrange("(p t) c -> p t c", t=4), in_=ut[b][:])
 
-        x_t = {}
-        h_t = {}
         cg = {}
-
-        def load_xh(b):
-            x_t[b] = keep.tile([128, 4, D], BF16, name="x%d" % b)
-            h_t[b] = keep.tile([128, 4, D], BF16, name="h%d" % b)
-            nc.sync.dma_start(out=x_t[b][:], in_=x[b].rearrange("(p t) c -> p t c", t=4))
-            nc.sync.dma_start(out=h_t[b][:], in_=h[b].rearrange("(p t) c -> p t c", t=4))
 
         def x_ilv(b, eng):
             cg[b] = pool.tile([128, 2 * D, 4], BF16, name="cg", bufs=3, align_bytes=64)
             interleave(eng, cg[b][:, 0:D, :], x_t[b][:])
-
-        rh = {}
-
-        def rh_mul(b, t, eng):
-            if b not in rh:
-                rh[b] = pool.tile([128, 4, D], F32, name="rh", bufs=2)
-            e = nc.gpsimd if eng == "G" else nc.vector
-            e.tensor_tensor(out=rh[b][:, t, :], in0=sig[b][:, t, 0:D], in1=h_t[b][:, t, :], op=MULT)
-
-        def store_rh(b):
-            nc.sync.dma_start(out=out_0[b].rearrange("(p t) c -> p t c", t=4), in_=rh[b][:])
 
         def rh_ilv(b, eng):
             interleave(eng, cg[b][:, D : 2 * D, :], rh[b][:])
@@ -227,27 +256,17 @@ def tile_dcgrucell_pb_kernel(
                 cs[b] = pool.tile([128, 2 * D], U8, name="cs", bufs=3, align_bytes=64)
             quantize(cc[b][:, c0:c1], cs[b][:, c0:c1], cg[b][:, c0:c1, :])
 
-        sup_raw = {}
         sup_grp = {}
         sup_codes = {}
         sup_sc = {}
 
-        def load_sup(s):
-            sup_raw[s] = keep.tile([128, 4, N], BF16, name="sup_raw%d" % s)
-            nc.sync.dma_start(out=sup_raw[s][:], in_=(support0, support1)[s].rearrange("(p t) k -> p t k", t=4))
-
-        def sup_unit(s, hh):
+        def sup_unit(s, hh, eng="S"):
             if hh == 0:
-                sup_grp[s] = pool.tile([128, N, 4], BF16, name="w_grp", bufs=2, align_bytes=64)
-            bank = psum.tile([128, 512], F32, name="tr")
-            for tt in range(2):
-                words = sup_raw[s][:, 2 * hh + tt, :].bitcast(F32)
-                for u in range(2):
-                    c = 256 * u + 128 * tt
-                    nc.tensor.transpose(bank[:, c : c + 128], words[:, u:256:2], ident[:])
-            dst = sup_grp[s][:, 256 * hh : 256 * (hh + 1), :].rearrange("p r t -> p (r t)").bitcast(F32)
-            nc.scalar.copy(
-                out=dst.rearrange("p (r u) -> p r u", u=2), in_=bank[:].rearrange("p (u r) -> p r u", u=2)
+                sup_grp[s] = pool.tile([128, N, 4], BF16, name="w_grp", bufs=3, align_bytes=64)
+            turn(
+                [sup_raw[s][:, 2 * hh + tt, :].bitcast(F32) for tt in range(2)],
+                sup_grp[s][:, 256 * hh : 256 * (hh + 1), :],
+                eng,
             )
 
         def q_sup(s):
@@ -259,7 +278,7 @@ def tile_dcgrucell_pb_kernel(
 
         def d1_tile(b, s):
             if (b, s) not in dt:
-                dt[(b, s)] = pool.tile([128, 4, 2 * D], F32, name="dt", bufs=3)
+                dt[(b, s)] = pool.tile([128, 4, 2 * D], F32, name="dt", bufs=4)
             return dt[(b, s)]
 
         def d1_mm(out, b, s, t, c0, c1):
@@ -279,12 +298,12 @@ def tile_dcgrucell_pb_kernel(
                 out=outs_d[s][b].rearrange("(p t) c -> p t c", t=4)[:, t0:t1, c0:c1], in_=dt[(b, s)][:, t0:t1, c0:c1]
             )
 
-        def d1_full(b, j):
+        def d1_full(b, j, eng="S"):
             s, t = divmod(j, 4)
             dtile = d1_tile(b, s)
             bank = psum.tile([128, 512], F32, name="tr")
             d1_mm(bank[:], b, s, t, 0, 2 * D)
-            nc.scalar.copy(out=dtile[:, t, :], in_=bank[:])
+            copy_out(eng, dtile[:, t, :], bank[:])
             if t == 3:
                 store_d1(b, s)
 
@@ -294,116 +313,115 @@ def tile_dcgrucell_pb_kernel(
             bank = psum.tile([128, 512], F32, name="tr")
             for q in range(2):
                 d1_mm(bank[:, D * q : D * (q + 1)], b, s, 2 * tp + q, c0, c0 + D)
-            dst = dtile[:, 2 * tp : 2 * tp + 2, c0 : c0 + D]
-            src = bank[:].rearrange("p (q c) -> p q c", q=2)
-            if eng == "S":
-                nc.scalar.copy(out=dst, in_=src)
-            if eng == "V":
-                nc.vector.tensor_copy(out=dst, in_=src)
+            copy_out(eng, dtile[:, 2 * tp : 2 * tp + 2, c0 : c0 + D], bank[:].rearrange("p (q c) -> p q c", q=2))
 
-        w_ilv(0, "V")
-        widen0(0)
-        transposes(0)
-        w_q(0)
-        widen0(1)
-        w_ilv(1, "V")
-        widen0(2)
         load_w(3)
-        w_ilv(2, "G", 4)
-        load_w(4)
-        nc.sync.dma_start(out=bias[:], in_=gate_b.partition_broadcast(128))
+        nc.sync.dma_start(out=brow[0:4, :], in_=gate_b.rearrange("(m q) -> m q", m=4))
         load_cat(1, 0)
         load_cat(1, 1)
-        load_sup(0)
-        load_sup(1)
-        load_xh(0)
-        load_cat(2, 0)
-        load_cat(2, 1)
-        load_xh(1)
-        load_xh(2)
-        load_xh(3)
-
-        NS = B * G
-        D1_AT = {}
-        for b in range(3):
-            for j in range(8):
-                D1_AT.setdefault(5 * b + 8 + (j // 2 if b < 2 else j // 4), []).append((b, j))
-
-        for i in range(NS):
-            b, g = divmod(i, G)
-            if b < 3 and g < 4:
-                widen(b + 1, g)
-            if b >= 1 and g == 1:
-                bias_add(b - 1, 0)
-                bias_add(b - 1, 1)
-            scale_evac(i, 0)
-            if i > 0:
-                q_cat(i - 1)
-            if i == 0:
+        D1 = {9: [(0, j) for j in range(4)], 10: [(0, j) for j in range(4, 8)], 14: [(1, j) for j in range(4)], 15: [(1, j) for j in range(4, 8)], 19: [(2, j) for j in range(4)], 20: [(2, j) for j in range(4, 8)]}
+        w_ilv(0, "S")
+        for j in range(NS + 2):
+            b, g = divmod(j, G)
+            if j < NS:
+                scaled(j, 0)
+                scaled(j, 1)
+            if j >= 2:
+                q_cat(j - 2)
+            if j == 1:
+                w_ilv(1, "V")
+                w_q(0)
+            if j == 2:
                 w_q(1)
-            if i == 1:
+            if j == 3:
                 w_q(2)
-                w_ilv(3, "S")
-                w_ilv(4, "G", 4)
-            if i == 2:
+            if j == 4:
                 w_q(3)
+            if j == 5:
+                w_q(4)
+            if j in (9, 14):
+                q_cand(b - 1)
+            if j == 6:
+                q_sup(0)
+            if j == 7:
+                q_sup(1)
+            if j == 11:
+                q_cand(3, 0, D)
+            if 1 <= j <= NS:
+                turn_cat(j - 1, 0, "S")
+                turn_cat(j - 1, 1, "V" if j == NS else "S")
+            if j < NS:
+                scaled(j, 2)
+                scaled(j, 3)
+            if j == 0:
+                w_ilv(2, "S")
+                load_w(4)
+                load_sup(0)
+                load_sup(1)
+                load_xh(0)
+                load_cat(2, 0)
+                load_cat(2, 1)
+                load_xh(3)
+                load_xh(1)
+                load_xh(2)
+            if j == 2:
+                w_ilv(3, "S")
+                bias_cols()
+            if j == 3:
+                w_ilv(4, "S")
+            if j == 10:
+                load_cat(3, 0)
+                load_cat(3, 1)
+            if j == 4:
                 sup_unit(0, 0)
                 sup_unit(0, 1)
-            if i == 2:
-                load_cat(3, 0)
-            if i == 3:
-                w_q(4)
-                q_sup(0)
+            if j == 5:
                 sup_unit(1, 0)
                 sup_unit(1, 1)
-            if i == 4:
-                load_cat(3, 1)
-                q_sup(1)
+            if j == 6:
                 x_ilv(0, "S")
-            if b >= 1 and g == 1:
-                bias_add(b - 1, 2)
-                bias_add(b - 1, 3)
-                for t in range(4):
-                    sigm(b - 1, t)
-                    rh_mul(b - 1, t, "G")
-                store_u(b - 1)
-                store_rh(b - 1)
-            scale_evac(i, 1)
-            if b >= 1 and g == 2:
-                rh_ilv(b - 1, "S")
-                if b < 3:
-                    x_ilv(b, "S")
-            if b >= 1 and g == 3:
-                q_cand(b - 1)
-            if i == 14:
+            if j == 8:
                 x_ilv(3, "S")
-            if i == 15:
-                q_cand(3, 0, D)
-            if i + 1 < NS:
-                transposes(i + 1)
-            if i > 0:
-                gates(i - 1)
-            for bb, j in D1_AT.get(i, ()):
-                d1_full(bb, j)
-            if i == 17:
-                for j in range(4):
-                    d1_half(3, j, 0, "S")
-
-        q_cat(NS - 1)
-        gates(NS - 1)
-        for t in range(4):
-            bias_add(3, t, 0, D)
-            sigm(3, t, 0, D)
-        for t in range(4):
-            rh_mul(3, t, "V")
+            if j == 11:
+                x_ilv(1, "S")
+            if j == 16:
+                x_ilv(2, "S")
+            if j >= 7 and g == 2:
+                for tp in range(2):
+                    rh_part(b - 1, tp)
+                store_rh(b - 1)
+            if j >= 2:
+                gates(j - 2)
+            if j >= 6 and g == 1 and j < NS + 1:
+                for m in range(4):
+                    sigm(b - 1, m)
+            if j >= 7 and g == 2:
+                for tp in range(2):
+                    u_part(b - 1, tp)
+                store_u(b - 1)
+                rh_ilv(b - 1, "S")
+            for bb, jj in D1.get(j, ()):
+                d1_full(bb, jj)
+            if j == 18:
+                q_cand(2)
+            if j == 16:
+                for jj in range(4):
+                    d1_half(3, jj, 0, "S")
+                    if jj % 2:
+                        store_d1(3, jj // 2, 0, D)
+        for m in range(2):
+            sigm(3, m)
+        for tp in range(2):
+            rh_part(3, tp)
         store_rh(3)
         rh_ilv(3, "V")
         q_cand(3, D, 2 * D)
-        for t in range(4):
-            bias_add(3, t, D, NG)
-            sigm(3, t, D, NG)
-        store_u(3)
+        for m in range(2, 4):
+            sigm(3, m)
         for j in range(4):
             d1_half(3, j, D, "V" if j % 2 else "S")
             if j % 2:
-                store_d1(3, j // 2)
+                store_d1(3, j // 2, D, 2 * D)
+        for tp in range(2):
+            u_part(3, tp, "VS"[tp])
+        store_u(3)

@@ -10,6 +10,7 @@ U8 = mybir.dt.uint8
 FP8 = mybir.dt.float8_e4m3fn
 FP8X4 = mybir.dt.float8_e4m3fn_x4
 MULT = mybir.AluOpType.mult
+ADD = mybir.AluOpType.add
 SIGMOID = mybir.ActivationFunctionType.Sigmoid
 
 B, N, F, D = 4, 512, 2560, 256
@@ -19,7 +20,386 @@ NS = B * G
 FLOPS = 2 * B * N * F * NG + 2 * 2 * B * N * N * 2 * D
 
 LOADS0 = ((0, 512), (512, 1536), (1536, 2560))
+CHUNKS = ((0, 1024), (1024, 2048), (2048, 2560))
 PAD = 64
+ORDER = (
+    (("WI", 0), "V"),
+    (("WD", 0, 0, 0), "S"),
+    (("WD", 0, 1, 0), "S"),
+    (("WD", 0, 2, 0), "S"),
+    (("WQ", 0), "V"),
+    (("TR", 0, 0), "PE"),
+    (("WD", 0, 3, 0), "S"),
+    (("WD", 0, 0, 1), "S"),
+    (("TR", 0, 1), "PE"),
+    (("EV", 0, 0), "V"),
+    (("WD", 0, 1, 1), "S"),
+    (("WD", 0, 2, 1), "S"),
+    (("EV", 0, 1), "V"),
+    (("TR", 1, 0), "PE"),
+    (("WD", 0, 3, 1), "S"),
+    (("WI", 1), "S"),
+    (("EV", 1, 0), "V"),
+    (("TR", 1, 1), "PE"),
+    (("TR", 2, 0), "PE"),
+    (("Q", 0), "V"),
+    (("TR", 2, 1), "PE"),
+    (("EV", 1, 1), "V"),
+    (("GM", 0, 0), "PE"),
+    (("GM", 0, 1), "PE"),
+    (("WD", 0, 0, 2), "S"),
+    (("GM", 0, 2), "PE"),
+    (("WI", 2), "V"),
+    (("GM", 0, 3), "PE"),
+    (("WD", 0, 1, 2), "S"),
+    (("WD", 0, 2, 2), "S"),
+    (("TR", 3, 0), "PE"),
+    (("WD", 0, 3, 2), "S"),
+    (("EV", 2, 1), "V"),
+    (("WI", 3), "S"),
+    (("TR", 3, 1), "PE"),
+    (("WQ", 2), "V"),
+    (("TR", 4, 0), "PE"),
+    (("EV", 2, 0), "V"),
+    (("Q", 1), "V"),
+    (("TR", 4, 1), "PE"),
+    (("WI", 4), "S"),
+    (("Q", 2), "V"),
+    (("WQ", 1), "V"),
+    (("EV", 3, 0), "V"),
+    (("GM", 1, 0), "PE"),
+    (("GM", 1, 1), "PE"),
+    (("WD", 1, 0, 0), "S"),
+    (("GM", 1, 2), "PE"),
+    (("EV", 3, 1), "V"),
+    (("ST", 0, 1), "PE"),
+    (("WD", 1, 1, 0), "S"),
+    (("WD", 1, 2, 0), "S"),
+    (("GM", 1, 3), "PE"),
+    (("EV", 4, 0), "V"),
+    (("TR", 5, 0), "PE"),
+    (("WD", 1, 3, 0), "S"),
+    (("XI", 0), "S"),
+    (("GM", 2, 0), "PE"),
+    (("EV", 4, 1), "V"),
+    (("TR", 5, 1), "PE"),
+    (("GM", 2, 1), "PE"),
+    (("WD", 1, 0, 1), "S"),
+    (("EV", 5, 1), "V"),
+    (("TR", 6, 0), "PE"),
+    (("WD", 1, 1, 1), "S"),
+    (("GM", 2, 2), "PE"),
+    (("WD", 1, 2, 1), "S"),
+    (("EV", 6, 0), "V"),
+    (("TR", 6, 1), "PE"),
+    (("WD", 1, 3, 1), "S"),
+    (("GM", 2, 3), "PE"),
+    (("WD", 1, 0, 2), "S"),
+    (("EV", 6, 1), "V"),
+    (("ST", 0, 0), "PE"),
+    (("WD", 1, 1, 2), "S"),
+    (("WD", 1, 2, 2), "S"),
+    (("WD", 1, 3, 2), "S"),
+    (("QX", 0), "V"),
+    (("XI", 1), "S"),
+    (("EV", 5, 0), "V"),
+    (("WD", 2, 0, 0), "S"),
+    (("WQ", 3), "V"),
+    (("WD", 2, 1, 0), "S"),
+    (("QX", 1), "V"),
+    (("ST", 1, 1), "PE"),
+    (("Q", 3), "V"),
+    (("WD", 2, 2, 0), "S"),
+    (("ST", 1, 0), "PE"),
+    (("WQ", 4), "V"),
+    (("WD", 2, 3, 0), "S"),
+    (("GM", 3, 1), "PE"),
+    (("Q", 4), "V"),
+    (("GM", 3, 0), "PE"),
+    (("SE", 0, 0), "S"),
+    (("GM", 3, 3), "PE"),
+    (("GM", 3, 2), "PE"),
+    (("SE", 1, 1), "S"),
+    (("Q", 5), "V"),
+    (("TR", 7, 0), "PE"),
+    (("XI", 2), "S"),
+    (("Q", 6), "V"),
+    (("TR", 7, 1), "PE"),
+    (("EV", 7, 0), "V"),
+    (("GM", 4, 1), "PE"),
+    (("XI", 3), "S"),
+    (("GM", 4, 0), "PE"),
+    (("GM", 4, 2), "PE"),
+    (("EV", 7, 1), "V"),
+    (("TR", 8, 0), "PE"),
+    (("SE", 1, 0), "S"),
+    (("GM", 4, 3), "PE"),
+    (("EV", 8, 0), "V"),
+    (("TR", 8, 1), "PE"),
+    (("WD", 2, 0, 1), "S"),
+    (("TR", 9, 0), "PE"),
+    (("WD", 2, 1, 1), "S"),
+    (("Q", 7), "V"),
+    (("TR", 9, 1), "PE"),
+    (("WD", 2, 2, 1), "S"),
+    (("EV", 9, 0), "V"),
+    (("WD", 2, 3, 1), "S"),
+    (("WD", 2, 0, 2), "S"),
+    (("WD", 2, 1, 2), "S"),
+    (("EV", 9, 1), "V"),
+    (("TR", 10, 0), "PE"),
+    (("WD", 2, 2, 2), "S"),
+    (("WD", 2, 3, 2), "S"),
+    (("SE", 0, 1), "S"),
+    (("EV", 10, 0), "V"),
+    (("TR", 10, 1), "PE"),
+    (("SG", 0, 0), "S"),
+    (("TR", 11, 0), "PE"),
+    (("SG", 0, 1), "S"),
+    (("SQ", 0), "V"),
+    (("TR", 11, 1), "PE"),
+    (("WD", 3, 0, 0), "S"),
+    (("EV", 11, 0), "V"),
+    (("GM", 5, 0), "PE"),
+    (("WD", 3, 1, 0), "S"),
+    (("GM", 6, 0), "PE"),
+    (("GM", 5, 1), "PE"),
+    (("WD", 3, 2, 0), "S"),
+    (("GM", 6, 1), "PE"),
+    (("EV", 11, 1), "V"),
+    (("GM", 7, 1), "PE"),
+    (("WD", 3, 3, 0), "S"),
+    (("GM", 7, 0), "PE"),
+    (("RT", 0, 0, 1), "PE"),
+    (("SG", 0, 2), "S"),
+    (("EV", 10, 1), "V"),
+    (("RT", 0, 0, 0), "PE"),
+    (("SG", 0, 3), "S"),
+    (("GM", 5, 2), "PE"),
+    (("GM", 6, 2), "PE"),
+    (("RM", 0, 0), "V"),
+    (("RT", 0, 1, 1), "PE"),
+    (("EV", 8, 1), "V"),
+    (("GM", 5, 3), "PE"),
+    (("UE", 0, 1), "S"),
+    (("GM", 6, 3), "PE"),
+    (("RT", 0, 1, 0), "PE"),
+    (("RM", 0, 1), "V"),
+    (("GM", 7, 2), "PE"),
+    (("UE", 0, 0), "S"),
+    (("GM", 7, 3), "PE"),
+    (("Q", 8), "V"),
+    (("RI", 0), "S"),
+    (("Q", 9), "V"),
+    (("TR", 12, 0), "PE"),
+    (("Q", 10), "V"),
+    (("TR", 12, 1), "PE"),
+    (("EV", 12, 0), "V"),
+    (("TR", 13, 0), "PE"),
+    (("TR", 13, 1), "PE"),
+    (("WD", 3, 0, 1), "S"),
+    (("EV", 12, 1), "V"),
+    (("TR", 14, 0), "PE"),
+    (("WD", 3, 1, 1), "S"),
+    (("GM", 8, 1), "PE"),
+    (("WD", 3, 2, 1), "S"),
+    (("GM", 9, 1), "PE"),
+    (("Q", 11), "V"),
+    (("WD", 3, 3, 1), "S"),
+    (("TR", 14, 1), "PE"),
+    (("EV", 13, 0), "V"),
+    (("WD", 3, 0, 2), "S"),
+    (("GM", 8, 0), "PE"),
+    (("WD", 3, 1, 2), "S"),
+    (("GM", 9, 0), "PE"),
+    (("WD", 3, 2, 2), "S"),
+    (("GM", 8, 3), "PE"),
+    (("WD", 3, 3, 2), "S"),
+    (("QR", 0), "V"),
+    (("TR", 15, 0), "PE"),
+    (("SG", 1, 0), "S"),
+    (("EV", 14, 1), "V"),
+    (("SG", 1, 1), "S"),
+    (("GM", 9, 3), "PE"),
+    (("GM", 10, 0), "PE"),
+    (("EV", 15, 0), "V"),
+    (("TR", 15, 1), "PE"),
+    (("GM", 10, 1), "PE"),
+    (("EV", 15, 1), "V"),
+    (("DM", 0, 0, 2), "PE"),
+    (("GM", 11, 0), "PE"),
+    (("DE", 0, 0, 2), "S"),
+    (("GM", 11, 1), "PE"),
+    (("GM", 8, 2), "PE"),
+    (("EV", 13, 1), "V"),
+    (("DM", 0, 0, 1), "PE"),
+    (("RT", 1, 0, 0), "PE"),
+    (("DE", 0, 0, 1), "S"),
+    (("GM", 9, 2), "PE"),
+    (("Q", 12), "V"),
+    (("RT", 1, 0, 1), "PE"),
+    (("SG", 1, 2), "S"),
+    (("RM", 1, 0), "V"),
+    (("TR", 16, 0), "PE"),
+    (("SG", 1, 3), "S"),
+    (("RM", 1, 1), "V"),
+    (("TR", 16, 1), "PE"),
+    (("EV", 16, 0), "V"),
+    (("GM", 12, 0), "PE"),
+    (("RI", 1), "S"),
+    (("GM", 12, 1), "PE"),
+    (("GM", 10, 2), "PE"),
+    (("GM", 10, 3), "PE"),
+    (("EV", 16, 1), "V"),
+    (("RT", 1, 1, 1), "PE"),
+    (("RT", 1, 1, 0), "PE"),
+    (("UE", 1, 1), "S"),
+    (("QR", 1), "V"),
+    (("GM", 11, 2), "PE"),
+    (("DM", 0, 0, 3), "PE"),
+    (("Q", 13), "V"),
+    (("UE", 1, 0), "S"),
+    (("DM", 1, 0, 2), "PE"),
+    (("QX", 2), "V"),
+    (("DE", 0, 0, 3), "S"),
+    (("DM", 1, 0, 1), "PE"),
+    (("EV", 14, 0), "V"),
+    (("GM", 13, 1), "PE"),
+    (("DE", 1, 0, 2), "S"),
+    (("TR", 17, 0), "PE"),
+    (("DE", 1, 0, 1), "S"),
+    (("TR", 17, 1), "PE"),
+    (("SQ", 1), "V"),
+    (("DM", 1, 0, 3), "PE"),
+    (("EV", 17, 0), "V"),
+    (("DM", 1, 1, 2), "PE"),
+    (("DE", 1, 0, 3), "S"),
+    (("GM", 13, 0), "PE"),
+    (("GM", 12, 2), "PE"),
+    (("DE", 1, 1, 2), "S"),
+    (("Q", 14), "V"),
+    (("DM", 1, 0, 0), "PE"),
+    (("DM", 1, 1, 3), "PE"),
+    (("DE", 1, 0, 0), "S"),
+    (("DM", 1, 1, 0), "PE"),
+    (("EV", 17, 1), "V"),
+    (("GM", 14, 1), "PE"),
+    (("DE", 1, 1, 0), "S"),
+    (("DM", 1, 1, 1), "PE"),
+    (("GM", 14, 0), "PE"),
+    (("DE", 1, 1, 3), "S"),
+    (("QX", 3), "V"),
+    (("TR", 18, 0), "PE"),
+    (("SG", 2, 0), "S"),
+    (("TR", 18, 1), "PE"),
+    (("EV", 18, 0), "V"),
+    (("SG", 2, 1), "S"),
+    (("DM", 3, 1, 2, 0), "PE"),
+    (("GM", 13, 2), "PE"),
+    (("DE", 1, 1, 1), "S"),
+    (("GM", 11, 3), "PE"),
+    (("EV", 18, 1), "V"),
+    (("DE", 3, 1, 2, 0), "S"),
+    (("RT", 2, 0, 0), "PE"),
+    (("DM", 3, 0, 0, 0), "PE"),
+    (("DM", 3, 0, 2, 0), "PE"),
+    (("RM", 2, 0), "V"),
+    (("DE", 3, 0, 0, 0), "S"),
+    (("DM", 3, 1, 0, 0), "PE"),
+    (("Q", 15), "V"),
+    (("DM", 0, 1, 2), "PE"),
+    (("DE", 3, 1, 0, 0), "S"),
+    (("RT", 2, 0, 1), "PE"),
+    (("DE", 3, 0, 2, 0), "V"),
+    (("DE", 0, 1, 2), "S"),
+    (("TR", 19, 0), "PE"),
+    (("RM", 2, 1), "V"),
+    (("TR", 19, 1), "PE"),
+    (("EV", 19, 0), "V"),
+    (("RI", 2), "S"),
+    (("DM", 0, 1, 0), "PE"),
+    (("DM", 0, 1, 1), "PE"),
+    (("GM", 15, 0), "PE"),
+    (("EV", 19, 1), "V"),
+    (("GM", 15, 1), "PE"),
+    (("DM", 0, 1, 3), "PE"),
+    (("DE", 0, 1, 0), "S"),
+    (("GM", 12, 3), "PE"),
+    (("GM", 13, 3), "PE"),
+    (("DE", 0, 1, 3), "S"),
+    (("Q", 16), "V"),
+    (("DM", 0, 0, 0), "PE"),
+    (("GM", 14, 3), "PE"),
+    (("DE", 0, 0, 0), "S"),
+    (("GM", 14, 2), "PE"),
+    (("Q", 17), "V"),
+    (("GM", 16, 1), "PE"),
+    (("DE", 0, 1, 1), "S"),
+    (("GM", 16, 0), "PE"),
+    (("Q", 18), "V"),
+    (("GM", 17, 1), "PE"),
+    (("GM", 17, 0), "PE"),
+    (("SG", 2, 2), "S"),
+    (("QR", 2), "V"),
+    (("GM", 18, 1), "PE"),
+    (("SG", 2, 3), "S"),
+    (("GM", 18, 0), "PE"),
+    (("GM", 15, 2), "PE"),
+    (("GM", 16, 2), "PE"),
+    (("RT", 2, 1, 1), "PE"),
+    (("RT", 2, 1, 0), "PE"),
+    (("UE", 2, 1), "S"),
+    (("GM", 15, 3), "PE"),
+    (("GM", 16, 3), "PE"),
+    (("Q", 19), "V"),
+    (("UE", 2, 0), "S"),
+    (("DM", 2, 0, 1), "PE"),
+    (("DM", 2, 1, 2), "PE"),
+    (("DE", 2, 0, 1), "V"),
+    (("GM", 19, 0), "PE"),
+    (("DE", 2, 1, 2), "S"),
+    (("DM", 2, 0, 0), "PE"),
+    (("DM", 2, 0, 3), "PE"),
+    (("DE", 2, 0, 0), "S"),
+    (("DM", 2, 1, 1), "PE"),
+    (("DE", 2, 0, 3), "V"),
+    (("DM", 2, 0, 2), "PE"),
+    (("DE", 2, 1, 1), "S"),
+    (("DM", 2, 1, 0), "PE"),
+    (("DE", 2, 0, 2), "V"),
+    (("DM", 2, 1, 3), "PE"),
+    (("DE", 2, 1, 0), "S"),
+    (("GM", 19, 1), "PE"),
+    (("DE", 2, 1, 3), "V"),
+    (("GM", 17, 2), "PE"),
+    (("SG", 3, 0), "S"),
+    (("GM", 18, 2), "PE"),
+    (("GM", 17, 3), "PE"),
+    (("SG", 3, 1), "S"),
+    (("GM", 18, 3), "PE"),
+    (("GM", 19, 3), "PE"),
+    (("GM", 19, 2), "PE"),
+    (("RT", 3, 0, 1), "PE"),
+    (("SG", 3, 2), "S"),
+    (("RT", 3, 0, 0), "PE"),
+    (("RM", 3, 1), "V"),
+    (("SG", 3, 3), "S"),
+    (("RM", 3, 0), "V"),
+    (("RT", 3, 1, 0), "PE"),
+    (("RT", 3, 1, 1), "PE"),
+    (("UE", 3, 0), "S"),
+    (("RI", 3), "V"),
+    (("UE", 3, 1), "S"),
+    (("QR", 3), "V"),
+    (("DM", 3, 1, 0, 1), "PE"),
+    (("DM", 3, 1, 2, 1), "PE"),
+    (("DE", 3, 1, 0, 1), "S"),
+    (("DM", 3, 0, 2, 1), "PE"),
+    (("DE", 3, 1, 2, 1), "V"),
+    (("DM", 3, 0, 0, 1), "PE"),
+    (("DE", 3, 0, 2, 1), "S"),
+    (("DE", 3, 0, 0, 1), "V"),
+)
 
 
 def tile_dcgrucell_pb_kernel(
@@ -32,21 +412,16 @@ def tile_dcgrucell_pb_kernel(
         keep = ctx.enter_context(tc.tile_pool(name="keep", bufs=1))
         pool = ctx.enter_context(tc.tile_pool(name="pool", bufs=2))
         psum = ctx.enter_context(tc.psum_pool(name="psum", bufs=4))
+        ctx.enter_context(tc.manual_schedule())
 
-        scale = {}
-
-        def load_scale(c):
-            k0, k1 = LOADS0[c]
-            scale[c] = keep.tile([128, k1 - k0], F32, name="scale%d" % c)
-            nc.sync.dma_start(
-                out=scale[c][:], in_=cat_s.rearrange("a b k -> (a b k)")[k0:k1].partition_broadcast(128)
-            )
+        scale = keep.tile([128, G, 4], F32, name="scale")
+        nc.sync.dma_start(out=scale[:], in_=cat_s.rearrange("a b (g p t) -> p (a b g) t", p=128, t=4))
 
         w_raw = {}
         raw = {}
 
         def load_w(g):
-            w_raw[g] = pool.tile([128, 4, NG], BF16, name="w_raw", bufs=3)
+            w_raw[g] = pool.tile([128, 4, NG], BF16, name="w_raw", bufs=5)
             nc.sync.dma_start(out=w_raw[g][:], in_=gate_w[512 * g : 512 * (g + 1), :].rearrange("(p j) n -> p j n", j=4))
 
         def load_cat0(c):
@@ -77,32 +452,54 @@ def tile_dcgrucell_pb_kernel(
             sup_raw[s] = keep.tile([128, 4, N], BF16, name="sup_raw%d" % s)
             nc.sync.dma_start(out=sup_raw[s][:], in_=(support0, support1)[s].rearrange("(p t) k -> p t k", t=4))
 
-        load_scale(0)
-        load_cat0(0)
+        brow = keep.tile([128, 128], BF16, name="brow")
+        nc.gpsimd.memset(brow[:], 0.0)
         load_w(0)
-        load_scale(1)
+        load_cat0(0)
         load_cat0(1)
         load_w(1)
-        load_scale(2)
         load_cat0(2)
         load_w(2)
+        nc.sync.dma_start(out=brow[0:4, :], in_=gate_b.rearrange("(m q) -> m q", m=4))
+        load_w(3)
+        load_w(4)
+        load_cat(1, 0)
+        load_cat(1, 1)
+        load_sup(0)
+        load_sup(1)
+        load_xh(0)
+        load_cat(2, 0)
+        load_cat(2, 1)
+        load_xh(3)
+        load_xh(1)
+        load_xh(2)
 
         ident = keep.tile([128, 128], F32, name="ident")
         make_identity(nc, ident[:])
-        brow = keep.tile([128, 128], BF16, name="brow")
-        nc.gpsimd.memset(brow[:], 0.0)
         warm = keep.tile([128, 1], F32, name="warm")
         warm_out = keep.tile([128, 1], F32, name="warm_out")
         nc.vector.memset(warm[:], 0.0)
         nc.scalar.activation(out=warm_out[:], in_=warm[:], func=SIGMOID)
 
         def interleave(eng, dst, src):
-            d_ = dst.rearrange("p (c i) t -> p c t i", i=4)
-            s_ = src.rearrange("p t (c i) -> p c t i", i=4)
-            if eng == "V":
-                nc.vector.tensor_copy(out=d_, in_=s_)
-            if eng == "S":
-                nc.scalar.copy(out=d_, in_=s_)
+            if eng == "G":
+                n = src.shape[2]
+                for c in range(0, n, 128):
+                    nc.gpsimd.tensor_scalar(
+                        out=dst[:, c : c + 128, :],
+                        in0=src[:, :, c : c + 128].rearrange("p t c -> p c t"),
+                        scalar1=1.0,
+                        scalar2=0.0,
+                        op0=MULT,
+                        op1=ADD,
+                    )
+            else:
+                d_ = dst.rearrange("p (c i) t -> p c t i", i=4)
+                s_ = src.rearrange("p t (c i) -> p c t i", i=4)
+                if eng == "V":
+                    nc.vector.tensor_copy(out=d_, in_=s_)
+                if eng == "S":
+                    nc.scalar.copy(out=d_, in_=s_)
 
         def quantize(codes, scales, grouped):
             nc.vector.quantize_mx(
@@ -124,18 +521,20 @@ def tile_dcgrucell_pb_kernel(
 
         wide = {}
 
-        def scaled(i, t):
+        def widen(b, t, ch):
+            k0, k1 = (LOADS0 if b == 0 else CHUNKS)[ch]
+            src = raw[(0, ch)][:, t, 0 : k1 - k0] if b == 0 else raw[(b, t // 2)][:, t % 2, k0:k1]
+            wide[(b, t, ch)] = pool.tile([128, 1024], BF16, name="wide", bufs=12)
+            nc.scalar.copy(out=wide[(b, t, ch)][:, 0 : k1 - k0], in_=src.bitcast(FP8))
+
+        def wide_words(i, t):
             b, g = divmod(i, G)
-            wide[(i, t)] = pool.tile([128, 512], BF16, name="wide", bufs=16)
-            c = (g + 1) // 2
-            k0 = 512 * g - LOADS0[c][0]
-            if b == 0:
-                src = raw[(0, c)][:, t, k0 : k0 + 512]
-            else:
-                src = raw[(b, t // 2)][:, t % 2, 512 * g : 512 * (g + 1)]
-            nc.vector.tensor_tensor(
-                out=wide[(i, t)][:], in0=src.bitcast(FP8), in1=scale[c][:, k0 : k0 + 512], op=MULT
-            )
+            chunks = LOADS0 if b == 0 else CHUNKS
+            ch = 0
+            while chunks[ch][1] <= 512 * g:
+                ch += 1
+            k0 = 512 * g - chunks[ch][0]
+            return wide[(b, t, ch)][:, k0 : k0 + 512].bitcast(F32)
 
         def copy_out(eng, out, in_):
             if eng == "V":
@@ -143,54 +542,77 @@ def tile_dcgrucell_pb_kernel(
             if eng == "S":
                 nc.scalar.copy(out=out, in_=in_)
 
-        def turn(words, grouped, eng):
-            bank = psum.tile([128, 512], F32, name="tr")
+        bank = {}
+
+        def turn(name, words):
+            bank[name] = psum.tile([128, 512], F32, name="tr")
             for tt in range(2):
                 for u in range(2):
                     c = 256 * u + 128 * tt
-                    nc.tensor.transpose(bank[:, c : c + 128], words[tt][:, u:256:2], ident[:])
+                    nc.tensor.transpose(bank[name][:, c : c + 128], words[tt][:, u:256:2], ident[:])
+
+        def words_out(eng, name, grouped):
             copy_out(
                 eng,
                 grouped.rearrange("p r t -> p (r t)").bitcast(F32).rearrange("p (r u) -> p r u", u=2),
-                bank[:].rearrange("p (u r) -> p r u", u=2),
+                bank[name][:].rearrange("p (u r) -> p r u", u=2),
             )
 
         grp = {}
+        cw = {}
 
-        def turn_cat(i, hh, eng):
+        def turn_cat(i, hh):
+            turn(("TR", i, hh), [wide_words(i, 2 * hh + tt) for tt in range(2)])
+
+        def words_cat(i, hh):
+            cw[i] = pool.tile([128, 256, 4], BF16, name="cw", bufs=2)
+            words_out("S", ("TR", i, hh), cw[i][:])
+
+        def scale_cat(i, hh, eng):
+            g = i % G
             if i not in grp:
-                grp[i] = pool.tile([128, 512, 4], BF16, name="grp", bufs=3, align_bytes=64)
-            turn(
-                [wide[(i, 2 * hh + tt)][:].bitcast(F32) for tt in range(2)],
-                grp[i][:, 256 * hh : 256 * (hh + 1), :],
-                eng,
-            )
+                grp[i] = pool.tile([128, 512, 4], BF16, name="grp", bufs=4, align_bytes=64)
+            if eng == "V":
+                src = bank[("TR", i, hh)][:].rearrange("p (u r) -> p u r", u=2).bitcast(BF16)
+                nc.vector.tensor_tensor(
+                    out=grp[i][:, 256 * hh : 256 * (hh + 1), :].rearrange("p r (u e) -> p r u e", u=2),
+                    in0=src.rearrange("p u (r e) -> p r u e", e=2),
+                    in1=scale[:, g, :].rearrange("p (u e) -> p u e", u=2).unsqueeze(1).to_broadcast([128, 256, 2, 2]),
+                    op=MULT,
+                )
+            else:
+                for q in range(0, 256, 128):
+                    nc.gpsimd.tensor_tensor(
+                        out=grp[i][:, 256 * hh + q : 256 * hh + q + 128, :],
+                        in0=cw[i][:, q : q + 128, :],
+                        in1=scale[:, g, :].unsqueeze(1).to_broadcast([128, 128, 4]),
+                        op=MULT,
+                    )
 
         codes = {}
         scb = {}
 
         def q_cat(i):
-            codes[i] = pool.tile([128, 512], U32, name="codes", bufs=3, align_bytes=64)
-            scb[i] = pool.tile([128, 512], U8, name="scb", bufs=3, align_bytes=64)
+            codes[i] = pool.tile([128, 512], U32, name="codes", bufs=4, align_bytes=64)
+            scb[i] = pool.tile([128, 512], U8, name="scb", bufs=4, align_bytes=64)
             quantize(codes[i][:], scb[i][:], grp[i][:])
 
         gate = {}
 
-        def gates(i):
+        def gates(i, m):
             b, g = divmod(i, G)
-            for m in range(4):
-                if g == 0:
-                    gate[(b, m)] = psum.tile([128, N], F32, name="gate")
-                c = slice(128 * m, 128 * (m + 1))
-                nc.tensor.matmul_mx(
-                    out=gate[(b, m)][:],
-                    lhsT=w_codes[g][:, c].bitcast(FP8X4),
-                    lhsT_scale=w_sc[g][:, c],
-                    rhs=codes[i][:].bitcast(FP8X4),
-                    rhs_scale=scb[i][:],
-                    start=(g == 0),
-                    stop=(g == G - 1),
-                )
+            if g == 0:
+                gate[(b, m)] = psum.tile([128, N], F32, name="gate")
+            c = slice(128 * m, 128 * (m + 1))
+            nc.tensor.matmul_mx(
+                out=gate[(b, m)][:],
+                lhsT=w_codes[g][:, c].bitcast(FP8X4),
+                lhsT_scale=w_sc[g][:, c],
+                rhs=codes[i][:].bitcast(FP8X4),
+                rhs_scale=scb[i][:],
+                start=(g == 0),
+                stop=(g == G - 1),
+            )
 
         bcol = keep.tile([128, 4], F32, name="bcol")
 
@@ -210,76 +632,81 @@ def tile_dcgrucell_pb_kernel(
             )
 
         def sig_turn(b, half, tp):
-            bank = psum.tile([128, 512], F32, name="tr")
+            name = ("RT", b, half, tp)
+            bank[name] = psum.tile([128, 512], F32, name="tr")
             for tt in range(2):
                 for mm in range(2):
                     c = 256 * tt + 128 * mm
                     n0 = 128 * (2 * tp + tt)
-                    nc.tensor.transpose(bank[:, c : c + 128], sig[(b, 2 * half + mm)][:, n0 : n0 + 128], ident[:])
-            return bank[:].rearrange("p (t c) -> p t c", t=2)
+                    nc.tensor.transpose(bank[name][:, c : c + 128], sig[(b, 2 * half + mm)][:, n0 : n0 + 128], ident[:])
 
         rh = {}
         ut = {}
+        done = {}
 
         def rh_part(b, tp):
             if b not in rh:
                 rh[b] = pool.tile([128, 4, D], F32, name="rh", bufs=2)
             t2 = slice(2 * tp, 2 * tp + 2)
-            nc.vector.tensor_tensor(out=rh[b][:, t2, :], in0=sig_turn(b, 0, tp), in1=h_t[b][:, t2, :], op=MULT)
+            nc.vector.tensor_tensor(
+                out=rh[b][:, t2, :],
+                in0=bank[("RT", b, 0, tp)][:].rearrange("p (t c) -> p t c", t=2),
+                in1=h_t[b][:, t2, :],
+                op=MULT,
+            )
+            done[(b, 0)] = done.get((b, 0), 0) + 1
+            if done[(b, 0)] == 2:
+                nc.sync.dma_start(out=out_0[b].rearrange("(p t) c -> p t c", t=4), in_=rh[b][:])
 
-        def u_part(b, tp, eng="S"):
+        def u_part(b, tp, eng):
             if b not in ut:
                 ut[b] = pool.tile([128, 4, D], F32, name="ut", bufs=2)
-            copy_out(eng, ut[b][:, 2 * tp : 2 * tp + 2, :], sig_turn(b, 1, tp))
+            copy_out(
+                eng,
+                ut[b][:, 2 * tp : 2 * tp + 2, :],
+                bank[("RT", b, 1, tp)][:].rearrange("p (t c) -> p t c", t=2),
+            )
+            done[(b, 1)] = done.get((b, 1), 0) + 1
+            if done[(b, 1)] == 2:
+                nc.sync.dma_start(out=out_1[b].rearrange("(p t) c -> p t c", t=4), in_=ut[b][:])
 
-        def store_rh(b):
-            nc.sync.dma_start(out=out_0[b].rearrange("(p t) c -> p t c", t=4), in_=rh[b][:])
-
-        def store_u(b):
-            nc.sync.dma_start(out=out_1[b].rearrange("(p t) c -> p t c", t=4), in_=ut[b][:])
-
-        cg = {}
+        cgx = {}
+        cgr = {}
 
         def x_ilv(b, eng):
-            cg[b] = pool.tile([128, 2 * D, 4], BF16, name="cg", bufs=3, align_bytes=64)
-            interleave(eng, cg[b][:, 0:D, :], x_t[b][:])
+            cgx[b] = pool.tile([128, D, 4], BF16, name="cgx", bufs=3, align_bytes=64)
+            interleave(eng, cgx[b][:], x_t[b][:])
 
         def rh_ilv(b, eng):
-            interleave(eng, cg[b][:, D : 2 * D, :], rh[b][:])
+            cgr[b] = pool.tile([128, D, 4], BF16, name="cgr", bufs=2, align_bytes=64)
+            interleave(eng, cgr[b][:], rh[b][:])
 
         cc = {}
         cs = {}
 
-        def q_cand(b, c0=0, c1=2 * D):
-            if b not in cc:
+        def q_cand(b, half):
+            if half == 0:
                 cc[b] = pool.tile([128, 2 * D], U32, name="cc", bufs=3, align_bytes=64)
                 cs[b] = pool.tile([128, 2 * D], U8, name="cs", bufs=3, align_bytes=64)
-            quantize(cc[b][:, c0:c1], cs[b][:, c0:c1], cg[b][:, c0:c1, :])
+            c = slice(D * half, D * (half + 1))
+            quantize(cc[b][:, c], cs[b][:, c], (cgx, cgr)[half][b][:])
 
         sup_grp = {}
         sup_codes = {}
         sup_sc = {}
 
-        def sup_unit(s, hh, eng="S"):
-            if hh == 0:
+        def sup_turn(s, hh):
+            turn(("ST", s, hh), [sup_raw[s][:, 2 * hh + tt, :].bitcast(F32) for tt in range(2)])
+
+        def sup_words(s, hh, eng):
+            if s not in sup_grp:
                 sup_grp[s] = pool.tile([128, N, 4], BF16, name="w_grp", bufs=3, align_bytes=64)
-            turn(
-                [sup_raw[s][:, 2 * hh + tt, :].bitcast(F32) for tt in range(2)],
-                sup_grp[s][:, 256 * hh : 256 * (hh + 1), :],
-                eng,
-            )
+            words_out(eng, ("ST", s, hh), sup_grp[s][:, 256 * hh : 256 * (hh + 1), :])
 
         def q_sup(s):
             sup_codes[s] = keep.tile([128, N], U32, name="sup_codes%d" % s, align_bytes=64)
             sup_sc[s] = keep.tile([128, N], U8, name="sup_sc%d" % s, align_bytes=64)
             quantize(sup_codes[s][:], sup_sc[s][:], sup_grp[s][:])
-
-        dt = {}
-
-        def d1_tile(b, s):
-            if (b, s) not in dt:
-                dt[(b, s)] = pool.tile([128, 4, 2 * D], F32, name="dt", bufs=4)
-            return dt[(b, s)]
 
         def d1_mm(out, b, s, t, c0, c1):
             c = slice(128 * t, 128 * (t + 1))
@@ -293,135 +720,93 @@ def tile_dcgrucell_pb_kernel(
                 stop=True,
             )
 
-        def store_d1(b, s, c0=0, c1=2 * D, t0=0, t1=4):
+        dt = {}
+
+        def d1(b, s, t):
+            name = ("DM", b, s, t)
+            bank[name] = psum.tile([128, 512], F32, name="tr")
+            d1_mm(bank[name][:], b, s, t, 0, 2 * D)
+
+        def d1_out(b, s, t, eng):
+            t0 = t - t % 2
+            key = (b, s, t0)
+            if key not in dt:
+                dt[key] = pool.tile([128, 2, 2 * D], F32, name="dt", bufs=5)
+            copy_out(eng, dt[key][:, t - t0, :], bank[("DM", b, s, t)][:])
+            done[key] = done.get(key, 0) + 1
+            if done[key] == 2:
+                nc.sync.dma_start(
+                    out=outs_d[s][b].rearrange("(p t) c -> p t c", t=4)[:, t0 : t0 + 2, :], in_=dt[key][:]
+                )
+
+        def d1_half(b, s, t, half):
+            name = ("DM", b, s, t, half)
+            bank[name] = psum.tile([128, 512], F32, name="tr")
+            for q in range(2):
+                d1_mm(bank[name][:, D * q : D * (q + 1)], b, s, t + q, D * half, D * (half + 1))
+
+        def d1_half_out(b, s, t, half, eng):
+            dh = pool.tile([128, 2, D], F32, name="dh", bufs=4)
+            copy_out(eng, dh[:], bank[("DM", b, s, t, half)][:].rearrange("p (q c) -> p q c", q=2))
             nc.sync.dma_start(
-                out=outs_d[s][b].rearrange("(p t) c -> p t c", t=4)[:, t0:t1, c0:c1], in_=dt[(b, s)][:, t0:t1, c0:c1]
+                out=outs_d[s][b].rearrange("(p t) c -> p t c", t=4)[:, t : t + 2, D * half : D * (half + 1)], in_=dh[:]
             )
 
-        def d1_full(b, j, eng="S"):
-            s, t = divmod(j, 4)
-            dtile = d1_tile(b, s)
-            bank = psum.tile([128, 512], F32, name="tr")
-            d1_mm(bank[:], b, s, t, 0, 2 * D)
-            copy_out(eng, dtile[:, t, :], bank[:])
-            if t == 3:
-                store_d1(b, s)
-
-        def d1_half(b, j, c0, eng):
-            s, tp = divmod(j, 2)
-            dtile = d1_tile(b, s)
-            bank = psum.tile([128, 512], F32, name="tr")
-            for q in range(2):
-                d1_mm(bank[:, D * q : D * (q + 1)], b, s, 2 * tp + q, c0, c0 + D)
-            copy_out(eng, dtile[:, 2 * tp : 2 * tp + 2, c0 : c0 + D], bank[:].rearrange("p (q c) -> p q c", q=2))
-
-        load_w(3)
-        nc.sync.dma_start(out=brow[0:4, :], in_=gate_b.rearrange("(m q) -> m q", m=4))
-        load_cat(1, 0)
-        load_cat(1, 1)
-        D1 = {9: [(0, j) for j in range(4)], 10: [(0, j) for j in range(4, 8)], 14: [(1, j) for j in range(4)], 15: [(1, j) for j in range(4, 8)], 19: [(2, j) for j in range(4)], 20: [(2, j) for j in range(4, 8)]}
-        w_ilv(0, "S")
-        for j in range(NS + 2):
-            b, g = divmod(j, G)
-            if j < NS:
-                scaled(j, 0)
-                scaled(j, 1)
-            if j >= 2:
-                q_cat(j - 2)
-            if j == 1:
-                w_ilv(1, "V")
-                w_q(0)
-            if j == 2:
-                w_q(1)
-            if j == 3:
-                w_q(2)
-            if j == 4:
-                w_q(3)
-            if j == 5:
-                w_q(4)
-            if j in (9, 14):
-                q_cand(b - 1)
-            if j == 6:
-                q_sup(0)
-            if j == 7:
-                q_sup(1)
-            if j == 11:
-                q_cand(3, 0, D)
-            if 1 <= j <= NS:
-                turn_cat(j - 1, 0, "S")
-                turn_cat(j - 1, 1, "V" if j == NS else "S")
-            if j < NS:
-                scaled(j, 2)
-                scaled(j, 3)
-            if j == 0:
-                w_ilv(2, "S")
-                load_w(4)
-                load_sup(0)
-                load_sup(1)
-                load_xh(0)
-                load_cat(2, 0)
-                load_cat(2, 1)
-                load_xh(3)
-                load_xh(1)
-                load_xh(2)
-            if j == 2:
-                w_ilv(3, "S")
+        def run(name, eng):
+            kind, a = name[0], name[1:]
+            if kind == "WI":
+                w_ilv(a[0], eng)
+            elif kind == "WQ":
+                w_q(a[0])
+            elif kind == "ST":
+                sup_turn(*a)
+            elif kind == "SE":
+                sup_words(a[0], a[1], eng)
+            elif kind == "SQ":
+                q_sup(a[0])
+            elif kind == "WD":
+                widen(*a)
+                if a[0] == 1:
+                    key = ("raw", a[1] // 2)
+                    done[key] = done.get(key, 0) + 1
+                    if done[key] == 6:
+                        load_cat(3, a[1] // 2)
+            elif kind == "TR":
+                turn_cat(*a)
+            elif kind == "EC":
+                words_cat(*a)
+            elif kind == "EV":
+                scale_cat(a[0], a[1], eng)
+            elif kind == "Q":
+                q_cat(a[0])
+            elif kind == "GM":
+                gates(*a)
+            elif kind == "SG":
+                sigm(*a)
+            elif kind == "RT":
+                sig_turn(*a)
+            elif kind == "RM":
+                rh_part(*a)
+            elif kind == "UE":
+                u_part(a[0], a[1], eng)
+            elif kind == "XI":
+                x_ilv(a[0], eng)
+            elif kind == "RI":
+                rh_ilv(a[0], eng)
+            elif kind == "QX":
+                q_cand(a[0], 0)
+            elif kind == "QR":
+                q_cand(a[0], 1)
+            elif kind == "DM" and len(a) == 3:
+                d1(*a)
+            elif kind == "DE" and len(a) == 3:
+                d1_out(a[0], a[1], a[2], eng)
+            elif kind == "DM":
+                d1_half(*a)
+            else:
+                d1_half_out(a[0], a[1], a[2], a[3], eng)
+            if kind == "Q" and a == (1,):
                 bias_cols()
-            if j == 3:
-                w_ilv(4, "S")
-            if j == 10:
-                load_cat(3, 0)
-                load_cat(3, 1)
-            if j == 4:
-                sup_unit(0, 0)
-                sup_unit(0, 1)
-            if j == 5:
-                sup_unit(1, 0)
-                sup_unit(1, 1)
-            if j == 6:
-                x_ilv(0, "S")
-            if j == 8:
-                x_ilv(3, "S")
-            if j == 11:
-                x_ilv(1, "S")
-            if j == 16:
-                x_ilv(2, "S")
-            if j >= 7 and g == 2:
-                for tp in range(2):
-                    rh_part(b - 1, tp)
-                store_rh(b - 1)
-            if j >= 2:
-                gates(j - 2)
-            if j >= 6 and g == 1 and j < NS + 1:
-                for m in range(4):
-                    sigm(b - 1, m)
-            if j >= 7 and g == 2:
-                for tp in range(2):
-                    u_part(b - 1, tp)
-                store_u(b - 1)
-                rh_ilv(b - 1, "S")
-            for bb, jj in D1.get(j, ()):
-                d1_full(bb, jj)
-            if j == 18:
-                q_cand(2)
-            if j == 16:
-                for jj in range(4):
-                    d1_half(3, jj, 0, "S")
-                    if jj % 2:
-                        store_d1(3, jj // 2, 0, D)
-        for m in range(2):
-            sigm(3, m)
-        for tp in range(2):
-            rh_part(3, tp)
-        store_rh(3)
-        rh_ilv(3, "V")
-        q_cand(3, D, 2 * D)
-        for m in range(2, 4):
-            sigm(3, m)
-        for j in range(4):
-            d1_half(3, j, D, "V" if j % 2 else "S")
-            if j % 2:
-                store_d1(3, j // 2, D, 2 * D)
-        for tp in range(2):
-            u_part(3, tp, "VS"[tp])
-        store_u(3)
+
+        for name, eng in ORDER:
+            run(name, eng)

from contextlib import ExitStack

import concourse.mybir as mybir
from concourse.masks import make_identity

F32 = mybir.dt.float32
BF16 = mybir.dt.bfloat16
U32 = mybir.dt.uint32
U8 = mybir.dt.uint8
FP8 = mybir.dt.float8_e4m3fn
FP8X4 = mybir.dt.float8_e4m3fn_x4
MULT = mybir.AluOpType.mult
ADD = mybir.AluOpType.add
SIGMOID = mybir.ActivationFunctionType.Sigmoid

B, N, F, D = 4, 512, 2560, 256
G = F // 512
NG = 2 * D
NS = B * G
FLOPS = 2 * B * N * F * NG + 2 * 2 * B * N * N * 2 * D

LOADS0 = ((0, 512), (512, 1536), (1536, 2560))
CHUNKS = ((0, 1024), (1024, 2048), (2048, 2560))
PAD = 64
ORDER = (
    (("WI", 0), "V"),
    (("WD", 0, 0, 0), "S"),
    (("WD", 0, 1, 0), "S"),
    (("WD", 0, 2, 0), "S"),
    (("WQ", 0), "V"),
    (("TR", 0, 0), "PE"),
    (("WD", 0, 3, 0), "S"),
    (("WD", 0, 0, 1), "S"),
    (("TR", 0, 1), "PE"),
    (("EV", 0, 0), "V"),
    (("WD", 0, 1, 1), "S"),
    (("WD", 0, 2, 1), "S"),
    (("EV", 0, 1), "V"),
    (("TR", 1, 0), "PE"),
    (("WD", 0, 3, 1), "S"),
    (("WI", 1), "S"),
    (("EV", 1, 0), "V"),
    (("TR", 1, 1), "PE"),
    (("TR", 2, 0), "PE"),
    (("Q", 0), "V"),
    (("TR", 2, 1), "PE"),
    (("EV", 1, 1), "V"),
    (("GM", 0, 0), "PE"),
    (("GM", 0, 1), "PE"),
    (("WD", 0, 0, 2), "S"),
    (("GM", 0, 2), "PE"),
    (("WI", 2), "V"),
    (("GM", 0, 3), "PE"),
    (("WD", 0, 1, 2), "S"),
    (("WD", 0, 2, 2), "S"),
    (("TR", 3, 0), "PE"),
    (("WD", 0, 3, 2), "S"),
    (("EV", 2, 1), "V"),
    (("WI", 3), "S"),
    (("TR", 3, 1), "PE"),
    (("WQ", 2), "V"),
    (("TR", 4, 0), "PE"),
    (("EV", 2, 0), "V"),
    (("Q", 1), "V"),
    (("TR", 4, 1), "PE"),
    (("WI", 4), "S"),
    (("Q", 2), "V"),
    (("WQ", 1), "V"),
    (("EV", 3, 0), "V"),
    (("GM", 1, 0), "PE"),
    (("GM", 1, 1), "PE"),
    (("WD", 1, 0, 0), "S"),
    (("GM", 1, 2), "PE"),
    (("EV", 3, 1), "V"),
    (("ST", 0, 1), "PE"),
    (("WD", 1, 1, 0), "S"),
    (("WD", 1, 2, 0), "S"),
    (("GM", 1, 3), "PE"),
    (("EV", 4, 0), "V"),
    (("TR", 5, 0), "PE"),
    (("WD", 1, 3, 0), "S"),
    (("XI", 0), "S"),
    (("GM", 2, 0), "PE"),
    (("EV", 4, 1), "V"),
    (("TR", 5, 1), "PE"),
    (("GM", 2, 1), "PE"),
    (("WD", 1, 0, 1), "S"),
    (("EV", 5, 1), "V"),
    (("TR", 6, 0), "PE"),
    (("WD", 1, 1, 1), "S"),
    (("GM", 2, 2), "PE"),
    (("WD", 1, 2, 1), "S"),
    (("EV", 6, 0), "V"),
    (("TR", 6, 1), "PE"),
    (("WD", 1, 3, 1), "S"),
    (("GM", 2, 3), "PE"),
    (("WD", 1, 0, 2), "S"),
    (("EV", 6, 1), "V"),
    (("ST", 0, 0), "PE"),
    (("WD", 1, 1, 2), "S"),
    (("WD", 1, 2, 2), "S"),
    (("WD", 1, 3, 2), "S"),
    (("QX", 0), "V"),
    (("XI", 1), "S"),
    (("EV", 5, 0), "V"),
    (("WD", 2, 0, 0), "S"),
    (("WQ", 3), "V"),
    (("WD", 2, 1, 0), "S"),
    (("QX", 1), "V"),
    (("ST", 1, 1), "PE"),
    (("Q", 3), "V"),
    (("WD", 2, 2, 0), "S"),
    (("ST", 1, 0), "PE"),
    (("WQ", 4), "V"),
    (("WD", 2, 3, 0), "S"),
    (("GM", 3, 1), "PE"),
    (("Q", 4), "V"),
    (("GM", 3, 0), "PE"),
    (("SE", 0, 0), "S"),
    (("GM", 3, 3), "PE"),
    (("GM", 3, 2), "PE"),
    (("SE", 1, 1), "S"),
    (("Q", 5), "V"),
    (("TR", 7, 0), "PE"),
    (("XI", 2), "S"),
    (("Q", 6), "V"),
    (("TR", 7, 1), "PE"),
    (("EV", 7, 0), "V"),
    (("GM", 4, 1), "PE"),
    (("XI", 3), "S"),
    (("GM", 4, 0), "PE"),
    (("GM", 4, 2), "PE"),
    (("EV", 7, 1), "V"),
    (("TR", 8, 0), "PE"),
    (("SE", 1, 0), "S"),
    (("GM", 4, 3), "PE"),
    (("EV", 8, 0), "V"),
    (("TR", 8, 1), "PE"),
    (("WD", 2, 0, 1), "S"),
    (("TR", 9, 0), "PE"),
    (("WD", 2, 1, 1), "S"),
    (("Q", 7), "V"),
    (("TR", 9, 1), "PE"),
    (("WD", 2, 2, 1), "S"),
    (("EV", 9, 0), "V"),
    (("WD", 2, 3, 1), "S"),
    (("WD", 2, 0, 2), "S"),
    (("WD", 2, 1, 2), "S"),
    (("EV", 9, 1), "V"),
    (("TR", 10, 0), "PE"),
    (("WD", 2, 2, 2), "S"),
    (("WD", 2, 3, 2), "S"),
    (("SE", 0, 1), "S"),
    (("EV", 10, 0), "V"),
    (("TR", 10, 1), "PE"),
    (("SG", 0, 0), "S"),
    (("TR", 11, 0), "PE"),
    (("SG", 0, 1), "S"),
    (("SQ", 0), "V"),
    (("TR", 11, 1), "PE"),
    (("WD", 3, 0, 0), "S"),
    (("EV", 11, 0), "V"),
    (("GM", 5, 0), "PE"),
    (("WD", 3, 1, 0), "S"),
    (("GM", 6, 0), "PE"),
    (("GM", 5, 1), "PE"),
    (("WD", 3, 2, 0), "S"),
    (("GM", 6, 1), "PE"),
    (("EV", 11, 1), "V"),
    (("GM", 7, 1), "PE"),
    (("WD", 3, 3, 0), "S"),
    (("GM", 7, 0), "PE"),
    (("RT", 0, 0, 1), "PE"),
    (("SG", 0, 2), "S"),
    (("EV", 10, 1), "V"),
    (("RT", 0, 0, 0), "PE"),
    (("SG", 0, 3), "S"),
    (("GM", 5, 2), "PE"),
    (("GM", 6, 2), "PE"),
    (("RM", 0, 0), "V"),
    (("RT", 0, 1, 1), "PE"),
    (("EV", 8, 1), "V"),
    (("GM", 5, 3), "PE"),
    (("UE", 0, 1), "S"),
    (("GM", 6, 3), "PE"),
    (("RT", 0, 1, 0), "PE"),
    (("RM", 0, 1), "V"),
    (("GM", 7, 2), "PE"),
    (("UE", 0, 0), "S"),
    (("GM", 7, 3), "PE"),
    (("Q", 8), "V"),
    (("RI", 0), "S"),
    (("Q", 9), "V"),
    (("TR", 12, 0), "PE"),
    (("Q", 10), "V"),
    (("TR", 12, 1), "PE"),
    (("EV", 12, 0), "V"),
    (("TR", 13, 0), "PE"),
    (("TR", 13, 1), "PE"),
    (("WD", 3, 0, 1), "S"),
    (("EV", 12, 1), "V"),
    (("TR", 14, 0), "PE"),
    (("WD", 3, 1, 1), "S"),
    (("GM", 8, 1), "PE"),
    (("WD", 3, 2, 1), "S"),
    (("GM", 9, 1), "PE"),
    (("Q", 11), "V"),
    (("WD", 3, 3, 1), "S"),
    (("TR", 14, 1), "PE"),
    (("EV", 13, 0), "V"),
    (("WD", 3, 0, 2), "S"),
    (("GM", 8, 0), "PE"),
    (("WD", 3, 1, 2), "S"),
    (("GM", 9, 0), "PE"),
    (("WD", 3, 2, 2), "S"),
    (("GM", 8, 3), "PE"),
    (("WD", 3, 3, 2), "S"),
    (("QR", 0), "V"),
    (("TR", 15, 0), "PE"),
    (("SG", 1, 0), "S"),
    (("EV", 14, 1), "V"),
    (("SG", 1, 1), "S"),
    (("GM", 9, 3), "PE"),
    (("GM", 10, 0), "PE"),
    (("EV", 15, 0), "V"),
    (("TR", 15, 1), "PE"),
    (("GM", 10, 1), "PE"),
    (("EV", 15, 1), "V"),
    (("DM", 0, 0, 2), "PE"),
    (("GM", 11, 0), "PE"),
    (("DE", 0, 0, 2), "S"),
    (("GM", 11, 1), "PE"),
    (("GM", 8, 2), "PE"),
    (("EV", 13, 1), "V"),
    (("DM", 0, 0, 1), "PE"),
    (("RT", 1, 0, 0), "PE"),
    (("DE", 0, 0, 1), "S"),
    (("GM", 9, 2), "PE"),
    (("Q", 12), "V"),
    (("RT", 1, 0, 1), "PE"),
    (("SG", 1, 2), "S"),
    (("RM", 1, 0), "V"),
    (("TR", 16, 0), "PE"),
    (("SG", 1, 3), "S"),
    (("RM", 1, 1), "V"),
    (("TR", 16, 1), "PE"),
    (("EV", 16, 0), "V"),
    (("GM", 12, 0), "PE"),
    (("RI", 1), "S"),
    (("GM", 12, 1), "PE"),
    (("GM", 10, 2), "PE"),
    (("GM", 10, 3), "PE"),
    (("EV", 16, 1), "V"),
    (("RT", 1, 1, 1), "PE"),
    (("RT", 1, 1, 0), "PE"),
    (("UE", 1, 1), "S"),
    (("QR", 1), "V"),
    (("GM", 11, 2), "PE"),
    (("DM", 0, 0, 3), "PE"),
    (("Q", 13), "V"),
    (("UE", 1, 0), "S"),
    (("DM", 1, 0, 2), "PE"),
    (("QX", 2), "V"),
    (("DE", 0, 0, 3), "S"),
    (("DM", 1, 0, 1), "PE"),
    (("EV", 14, 0), "V"),
    (("GM", 13, 1), "PE"),
    (("DE", 1, 0, 2), "S"),
    (("TR", 17, 0), "PE"),
    (("DE", 1, 0, 1), "S"),
    (("TR", 17, 1), "PE"),
    (("SQ", 1), "V"),
    (("DM", 1, 0, 3), "PE"),
    (("EV", 17, 0), "V"),
    (("DM", 1, 1, 2), "PE"),
    (("DE", 1, 0, 3), "S"),
    (("GM", 13, 0), "PE"),
    (("GM", 12, 2), "PE"),
    (("DE", 1, 1, 2), "S"),
    (("Q", 14), "V"),
    (("DM", 1, 0, 0), "PE"),
    (("DM", 1, 1, 3), "PE"),
    (("DE", 1, 0, 0), "S"),
    (("DM", 1, 1, 0), "PE"),
    (("EV", 17, 1), "V"),
    (("GM", 14, 1), "PE"),
    (("DE", 1, 1, 0), "S"),
    (("DM", 1, 1, 1), "PE"),
    (("GM", 14, 0), "PE"),
    (("DE", 1, 1, 3), "S"),
    (("QX", 3), "V"),
    (("TR", 18, 0), "PE"),
    (("SG", 2, 0), "S"),
    (("TR", 18, 1), "PE"),
    (("EV", 18, 0), "V"),
    (("SG", 2, 1), "S"),
    (("DM", 3, 1, 2, 0), "PE"),
    (("GM", 13, 2), "PE"),
    (("DE", 1, 1, 1), "S"),
    (("GM", 11, 3), "PE"),
    (("EV", 18, 1), "V"),
    (("DE", 3, 1, 2, 0), "S"),
    (("RT", 2, 0, 0), "PE"),
    (("DM", 3, 0, 0, 0), "PE"),
    (("DM", 3, 0, 2, 0), "PE"),
    (("RM", 2, 0), "V"),
    (("DE", 3, 0, 0, 0), "S"),
    (("DM", 3, 1, 0, 0), "PE"),
    (("Q", 15), "V"),
    (("DM", 0, 1, 2), "PE"),
    (("DE", 3, 1, 0, 0), "S"),
    (("RT", 2, 0, 1), "PE"),
    (("DE", 3, 0, 2, 0), "V"),
    (("DE", 0, 1, 2), "S"),
    (("TR", 19, 0), "PE"),
    (("RM", 2, 1), "V"),
    (("TR", 19, 1), "PE"),
    (("EV", 19, 0), "V"),
    (("RI", 2), "S"),
    (("DM", 0, 1, 0), "PE"),
    (("DM", 0, 1, 1), "PE"),
    (("GM", 15, 0), "PE"),
    (("EV", 19, 1), "V"),
    (("GM", 15, 1), "PE"),
    (("DM", 0, 1, 3), "PE"),
    (("DE", 0, 1, 0), "S"),
    (("GM", 12, 3), "PE"),
    (("GM", 13, 3), "PE"),
    (("DE", 0, 1, 3), "S"),
    (("Q", 16), "V"),
    (("DM", 0, 0, 0), "PE"),
    (("GM", 14, 3), "PE"),
    (("DE", 0, 0, 0), "S"),
    (("GM", 14, 2), "PE"),
    (("Q", 17), "V"),
    (("GM", 16, 1), "PE"),
    (("DE", 0, 1, 1), "S"),
    (("GM", 16, 0), "PE"),
    (("Q", 18), "V"),
    (("GM", 17, 1), "PE"),
    (("GM", 17, 0), "PE"),
    (("SG", 2, 2), "S"),
    (("QR", 2), "V"),
    (("GM", 18, 1), "PE"),
    (("SG", 2, 3), "S"),
    (("GM", 18, 0), "PE"),
    (("GM", 15, 2), "PE"),
    (("GM", 16, 2), "PE"),
    (("RT", 2, 1, 1), "PE"),
    (("RT", 2, 1, 0), "PE"),
    (("UE", 2, 1), "S"),
    (("GM", 15, 3), "PE"),
    (("GM", 16, 3), "PE"),
    (("Q", 19), "V"),
    (("UE", 2, 0), "S"),
    (("DM", 2, 0, 1), "PE"),
    (("DM", 2, 1, 2), "PE"),
    (("DE", 2, 0, 1), "V"),
    (("GM", 19, 0), "PE"),
    (("DE", 2, 1, 2), "S"),
    (("DM", 2, 0, 0), "PE"),
    (("DM", 2, 0, 3), "PE"),
    (("DE", 2, 0, 0), "S"),
    (("DM", 2, 1, 1), "PE"),
    (("DE", 2, 0, 3), "V"),
    (("DM", 2, 0, 2), "PE"),
    (("DE", 2, 1, 1), "S"),
    (("DM", 2, 1, 0), "PE"),
    (("DE", 2, 0, 2), "V"),
    (("DM", 2, 1, 3), "PE"),
    (("DE", 2, 1, 0), "S"),
    (("GM", 19, 1), "PE"),
    (("DE", 2, 1, 3), "V"),
    (("GM", 17, 2), "PE"),
    (("SG", 3, 0), "S"),
    (("GM", 18, 2), "PE"),
    (("GM", 17, 3), "PE"),
    (("SG", 3, 1), "S"),
    (("GM", 18, 3), "PE"),
    (("GM", 19, 3), "PE"),
    (("GM", 19, 2), "PE"),
    (("RT", 3, 0, 1), "PE"),
    (("SG", 3, 2), "S"),
    (("RT", 3, 0, 0), "PE"),
    (("RM", 3, 1), "V"),
    (("SG", 3, 3), "S"),
    (("RM", 3, 0), "V"),
    (("RT", 3, 1, 0), "PE"),
    (("RT", 3, 1, 1), "PE"),
    (("UE", 3, 0), "S"),
    (("RI", 3), "V"),
    (("UE", 3, 1), "S"),
    (("QR", 3), "V"),
    (("DM", 3, 1, 0, 1), "PE"),
    (("DM", 3, 1, 2, 1), "PE"),
    (("DE", 3, 1, 0, 1), "S"),
    (("DM", 3, 0, 2, 1), "PE"),
    (("DE", 3, 1, 2, 1), "V"),
    (("DM", 3, 0, 0, 1), "PE"),
    (("DE", 3, 0, 2, 1), "S"),
    (("DE", 3, 0, 0, 1), "V"),
)


def tile_dcgrucell_pb_kernel(
    tc, cat_b, cat_s, gate_w, gate_b, x, h, support0, support1, out_0, out_1, out_2, out_3
):
    nc = tc.nc
    outs_d = (out_2, out_3)

    with ExitStack() as ctx:
        keep = ctx.enter_context(tc.tile_pool(name="keep", bufs=1))
        pool = ctx.enter_context(tc.tile_pool(name="pool", bufs=2))
        psum = ctx.enter_context(tc.psum_pool(name="psum", bufs=4))
        ctx.enter_context(tc.manual_schedule())

        scale = keep.tile([128, G, 4], F32, name="scale")
        nc.sync.dma_start(out=scale[:], in_=cat_s.rearrange("a b (g p t) -> p (a b g) t", p=128, t=4))

        w_raw = {}
        raw = {}

        def load_w(g):
            w_raw[g] = pool.tile([128, 4, NG], BF16, name="w_raw", bufs=5)
            nc.sync.dma_start(out=w_raw[g][:], in_=gate_w[512 * g : 512 * (g + 1), :].rearrange("(p j) n -> p j n", j=4))

        def load_cat0(c):
            k0, k1 = LOADS0[c]
            t_ = keep.tile([128, 4, k1 - k0 + PAD], U8, name="raw0_%d" % c, align_bytes=64)
            nc.sync.dma_start(out=t_[:, :, 0 : k1 - k0], in_=cat_b[0].rearrange("(p t) k -> p t k", t=4)[:, :, k0:k1])
            raw[(0, c)] = t_

        def load_cat(b, hh):
            t_ = pool.tile([128, 2, F + PAD], U8, name="raw", bufs=4, align_bytes=64)
            nc.sync.dma_start(
                out=t_[:, :, 0:F], in_=cat_b[b].rearrange("(p t) k -> p t k", t=4)[:, 2 * hh : 2 * hh + 2, :]
            )
            raw[(b, hh)] = t_

        x_t = {}
        h_t = {}

        def load_xh(b):
            x_t[b] = keep.tile([128, 4, D], BF16, name="x%d" % b)
            h_t[b] = keep.tile([128, 4, D], BF16, name="h%d" % b)
            nc.sync.dma_start(out=x_t[b][:], in_=x[b].rearrange("(p t) c -> p t c", t=4))
            nc.sync.dma_start(out=h_t[b][:], in_=h[b].rearrange("(p t) c -> p t c", t=4))

        sup_raw = {}

        def load_sup(s):
            sup_raw[s] = keep.tile([128, 4, N], BF16, name="sup_raw%d" % s)
            nc.sync.dma_start(out=sup_raw[s][:], in_=(support0, support1)[s].rearrange("(p t) k -> p t k", t=4))

        brow = keep.tile([128, 128], BF16, name="brow")
        nc.gpsimd.memset(brow[:], 0.0)
        load_w(0)
        load_cat0(0)
        load_cat0(1)
        load_w(1)
        load_cat0(2)
        load_w(2)
        nc.sync.dma_start(out=brow[0:4, :], in_=gate_b.rearrange("(m q) -> m q", m=4))
        load_w(3)
        load_w(4)
        load_cat(1, 0)
        load_cat(1, 1)
        load_sup(0)
        load_sup(1)
        load_xh(0)
        load_cat(2, 0)
        load_cat(2, 1)
        load_xh(3)
        load_xh(1)
        load_xh(2)

        ident = keep.tile([128, 128], F32, name="ident")
        make_identity(nc, ident[:])
        warm = keep.tile([128, 1], F32, name="warm")
        warm_out = keep.tile([128, 1], F32, name="warm_out")
        nc.vector.memset(warm[:], 0.0)
        nc.scalar.activation(out=warm_out[:], in_=warm[:], func=SIGMOID)

        def interleave(eng, dst, src):
            if eng == "G":
                n = src.shape[2]
                for c in range(0, n, 128):
                    nc.gpsimd.tensor_scalar(
                        out=dst[:, c : c + 128, :],
                        in0=src[:, :, c : c + 128].rearrange("p t c -> p c t"),
                        scalar1=1.0,
                        scalar2=0.0,
                        op0=MULT,
                        op1=ADD,
                    )
            else:
                d_ = dst.rearrange("p (c i) t -> p c t i", i=4)
                s_ = src.rearrange("p t (c i) -> p c t i", i=4)
                if eng == "V":
                    nc.vector.tensor_copy(out=d_, in_=s_)
                if eng == "S":
                    nc.scalar.copy(out=d_, in_=s_)

        def quantize(codes, scales, grouped):
            nc.vector.quantize_mx(
                out=codes.bitcast(FP8X4), scales=scales, in_=grouped.rearrange("p c t -> p (c t)")
            )

        w_grp = {}
        w_codes = {}
        w_sc = {}

        def w_ilv(g, eng):
            w_grp[g] = pool.tile([128, NG, 4], BF16, name="w_grp", bufs=3, align_bytes=64)
            interleave(eng, w_grp[g][:], w_raw[g][:])

        def w_q(g):
            w_codes[g] = keep.tile([128, NG], U32, name="w_codes%d" % g, align_bytes=64)
            w_sc[g] = keep.tile([128, NG], U8, name="w_sc%d" % g, align_bytes=64)
            quantize(w_codes[g][:], w_sc[g][:], w_grp[g][:])

        wide = {}

        def widen(b, t, ch):
            k0, k1 = (LOADS0 if b == 0 else CHUNKS)[ch]
            src = raw[(0, ch)][:, t, 0 : k1 - k0] if b == 0 else raw[(b, t // 2)][:, t % 2, k0:k1]
            wide[(b, t, ch)] = pool.tile([128, 1024], BF16, name="wide", bufs=12)
            nc.scalar.copy(out=wide[(b, t, ch)][:, 0 : k1 - k0], in_=src.bitcast(FP8))

        def wide_words(i, t):
            b, g = divmod(i, G)
            chunks = LOADS0 if b == 0 else CHUNKS
            ch = 0
            while chunks[ch][1] <= 512 * g:
                ch += 1
            k0 = 512 * g - chunks[ch][0]
            return wide[(b, t, ch)][:, k0 : k0 + 512].bitcast(F32)

        def copy_out(eng, out, in_):
            if eng == "V":
                nc.vector.tensor_copy(out=out, in_=in_)
            if eng == "S":
                nc.scalar.copy(out=out, in_=in_)

        bank = {}

        def turn(name, words):
            bank[name] = psum.tile([128, 512], F32, name="tr")
            for tt in range(2):
                for u in range(2):
                    c = 256 * u + 128 * tt
                    nc.tensor.transpose(bank[name][:, c : c + 128], words[tt][:, u:256:2], ident[:])

        def words_out(eng, name, grouped):
            copy_out(
                eng,
                grouped.rearrange("p r t -> p (r t)").bitcast(F32).rearrange("p (r u) -> p r u", u=2),
                bank[name][:].rearrange("p (u r) -> p r u", u=2),
            )

        grp = {}
        cw = {}

        def turn_cat(i, hh):
            turn(("TR", i, hh), [wide_words(i, 2 * hh + tt) for tt in range(2)])

        def words_cat(i, hh):
            cw[i] = pool.tile([128, 256, 4], BF16, name="cw", bufs=2)
            words_out("S", ("TR", i, hh), cw[i][:])

        def scale_cat(i, hh, eng):
            g = i % G
            if i not in grp:
                grp[i] = pool.tile([128, 512, 4], BF16, name="grp", bufs=4, align_bytes=64)
            if eng == "V":
                src = bank[("TR", i, hh)][:].rearrange("p (u r) -> p u r", u=2).bitcast(BF16)
                nc.vector.tensor_tensor(
                    out=grp[i][:, 256 * hh : 256 * (hh + 1), :].rearrange("p r (u e) -> p r u e", u=2),
                    in0=src.rearrange("p u (r e) -> p r u e", e=2),
                    in1=scale[:, g, :].rearrange("p (u e) -> p u e", u=2).unsqueeze(1).to_broadcast([128, 256, 2, 2]),
                    op=MULT,
                )
            else:
                for q in range(0, 256, 128):
                    nc.gpsimd.tensor_tensor(
                        out=grp[i][:, 256 * hh + q : 256 * hh + q + 128, :],
                        in0=cw[i][:, q : q + 128, :],
                        in1=scale[:, g, :].unsqueeze(1).to_broadcast([128, 128, 4]),
                        op=MULT,
                    )

        codes = {}
        scb = {}

        def q_cat(i):
            codes[i] = pool.tile([128, 512], U32, name="codes", bufs=4, align_bytes=64)
            scb[i] = pool.tile([128, 512], U8, name="scb", bufs=4, align_bytes=64)
            quantize(codes[i][:], scb[i][:], grp[i][:])

        gate = {}

        def gates(i, m):
            b, g = divmod(i, G)
            if g == 0:
                gate[(b, m)] = psum.tile([128, N], F32, name="gate")
            c = slice(128 * m, 128 * (m + 1))
            nc.tensor.matmul_mx(
                out=gate[(b, m)][:],
                lhsT=w_codes[g][:, c].bitcast(FP8X4),
                lhsT_scale=w_sc[g][:, c],
                rhs=codes[i][:].bitcast(FP8X4),
                rhs_scale=scb[i][:],
                start=(g == 0),
                stop=(g == G - 1),
            )

        bcol = keep.tile([128, 4], F32, name="bcol")

        def bias_cols():
            bf = keep.tile([128, 128], F32, name="bf")
            nc.vector.tensor_copy(out=bf[:], in_=brow[:])
            bank = psum.tile([128, 512], F32, name="tr")
            nc.tensor.transpose(bank[:, 0:128], bf[:], ident[:])
            nc.vector.tensor_copy(out=bcol[:], in_=bank[:, 0:4])

        sig = {}

        def sigm(b, m):
            sig[(b, m)] = pool.tile([128, N], F32, name="sig", bufs=6)
            nc.scalar.activation(
                out=sig[(b, m)][:], in_=gate[(b, m)][:], func=SIGMOID, bias=bcol[:, m : m + 1]
            )

        def sig_turn(b, half, tp):
            name = ("RT", b, half, tp)
            bank[name] = psum.tile([128, 512], F32, name="tr")
            for tt in range(2):
                for mm in range(2):
                    c = 256 * tt + 128 * mm
                    n0 = 128 * (2 * tp + tt)
                    nc.tensor.transpose(bank[name][:, c : c + 128], sig[(b, 2 * half + mm)][:, n0 : n0 + 128], ident[:])

        rh = {}
        ut = {}
        done = {}

        def rh_part(b, tp):
            if b not in rh:
                rh[b] = pool.tile([128, 4, D], F32, name="rh", bufs=2)
            t2 = slice(2 * tp, 2 * tp + 2)
            nc.vector.tensor_tensor(
                out=rh[b][:, t2, :],
                in0=bank[("RT", b, 0, tp)][:].rearrange("p (t c) -> p t c", t=2),
                in1=h_t[b][:, t2, :],
                op=MULT,
            )
            done[(b, 0)] = done.get((b, 0), 0) + 1
            if done[(b, 0)] == 2:
                nc.sync.dma_start(out=out_0[b].rearrange("(p t) c -> p t c", t=4), in_=rh[b][:])

        def u_part(b, tp, eng):
            if b not in ut:
                ut[b] = pool.tile([128, 4, D], F32, name="ut", bufs=2)
            copy_out(
                eng,
                ut[b][:, 2 * tp : 2 * tp + 2, :],
                bank[("RT", b, 1, tp)][:].rearrange("p (t c) -> p t c", t=2),
            )
            done[(b, 1)] = done.get((b, 1), 0) + 1
            if done[(b, 1)] == 2:
                nc.sync.dma_start(out=out_1[b].rearrange("(p t) c -> p t c", t=4), in_=ut[b][:])

        cgx = {}
        cgr = {}

        def x_ilv(b, eng):
            cgx[b] = pool.tile([128, D, 4], BF16, name="cgx", bufs=3, align_bytes=64)
            interleave(eng, cgx[b][:], x_t[b][:])

        def rh_ilv(b, eng):
            cgr[b] = pool.tile([128, D, 4], BF16, name="cgr", bufs=2, align_bytes=64)
            interleave(eng, cgr[b][:], rh[b][:])

        cc = {}
        cs = {}

        def q_cand(b, half):
            if half == 0:
                cc[b] = pool.tile([128, 2 * D], U32, name="cc", bufs=3, align_bytes=64)
                cs[b] = pool.tile([128, 2 * D], U8, name="cs", bufs=3, align_bytes=64)
            c = slice(D * half, D * (half + 1))
            quantize(cc[b][:, c], cs[b][:, c], (cgx, cgr)[half][b][:])

        sup_grp = {}
        sup_codes = {}
        sup_sc = {}

        def sup_turn(s, hh):
            turn(("ST", s, hh), [sup_raw[s][:, 2 * hh + tt, :].bitcast(F32) for tt in range(2)])

        def sup_words(s, hh, eng):
            if s not in sup_grp:
                sup_grp[s] = pool.tile([128, N, 4], BF16, name="w_grp", bufs=3, align_bytes=64)
            words_out(eng, ("ST", s, hh), sup_grp[s][:, 256 * hh : 256 * (hh + 1), :])

        def q_sup(s):
            sup_codes[s] = keep.tile([128, N], U32, name="sup_codes%d" % s, align_bytes=64)
            sup_sc[s] = keep.tile([128, N], U8, name="sup_sc%d" % s, align_bytes=64)
            quantize(sup_codes[s][:], sup_sc[s][:], sup_grp[s][:])

        def d1_mm(out, b, s, t, c0, c1):
            c = slice(128 * t, 128 * (t + 1))
            nc.tensor.matmul_mx(
                out=out,
                lhsT=sup_codes[s][:, c].bitcast(FP8X4),
                lhsT_scale=sup_sc[s][:, c],
                rhs=cc[b][:, c0:c1].bitcast(FP8X4),
                rhs_scale=cs[b][:, c0:c1],
                start=True,
                stop=True,
            )

        dt = {}

        def d1(b, s, t):
            name = ("DM", b, s, t)
            bank[name] = psum.tile([128, 512], F32, name="tr")
            d1_mm(bank[name][:], b, s, t, 0, 2 * D)

        def d1_out(b, s, t, eng):
            t0 = t - t % 2
            key = (b, s, t0)
            if key not in dt:
                dt[key] = pool.tile([128, 2, 2 * D], F32, name="dt", bufs=5)
            copy_out(eng, dt[key][:, t - t0, :], bank[("DM", b, s, t)][:])
            done[key] = done.get(key, 0) + 1
            if done[key] == 2:
                nc.sync.dma_start(
                    out=outs_d[s][b].rearrange("(p t) c -> p t c", t=4)[:, t0 : t0 + 2, :], in_=dt[key][:]
                )

        def d1_half(b, s, t, half):
            name = ("DM", b, s, t, half)
            bank[name] = psum.tile([128, 512], F32, name="tr")
            for q in range(2):
                d1_mm(bank[name][:, D * q : D * (q + 1)], b, s, t + q, D * half, D * (half + 1))

        def d1_half_out(b, s, t, half, eng):
            dh = pool.tile([128, 2, D], F32, name="dh", bufs=4)
            copy_out(eng, dh[:], bank[("DM", b, s, t, half)][:].rearrange("p (q c) -> p q c", q=2))
            nc.sync.dma_start(
                out=outs_d[s][b].rearrange("(p t) c -> p t c", t=4)[:, t : t + 2, D * half : D * (half + 1)], in_=dh[:]
            )

        def run(name, eng):
            kind, a = name[0], name[1:]
            if kind == "WI":
                w_ilv(a[0], eng)
            elif kind == "WQ":
                w_q(a[0])
            elif kind == "ST":
                sup_turn(*a)
            elif kind == "SE":
                sup_words(a[0], a[1], eng)
            elif kind == "SQ":
                q_sup(a[0])
            elif kind == "WD":
                widen(*a)
                if a[0] == 1:
                    key = ("raw", a[1] // 2)
                    done[key] = done.get(key, 0) + 1
                    if done[key] == 6:
                        load_cat(3, a[1] // 2)
            elif kind == "TR":
                turn_cat(*a)
            elif kind == "EC":
                words_cat(*a)
            elif kind == "EV":
                scale_cat(a[0], a[1], eng)
            elif kind == "Q":
                q_cat(a[0])
            elif kind == "GM":
                gates(*a)
            elif kind == "SG":
                sigm(*a)
            elif kind == "RT":
                sig_turn(*a)
            elif kind == "RM":
                rh_part(*a)
            elif kind == "UE":
                u_part(a[0], a[1], eng)
            elif kind == "XI":
                x_ilv(a[0], eng)
            elif kind == "RI":
                rh_ilv(a[0], eng)
            elif kind == "QX":
                q_cand(a[0], 0)
            elif kind == "QR":
                q_cand(a[0], 1)
            elif kind == "DM" and len(a) == 3:
                d1(*a)
            elif kind == "DE" and len(a) == 3:
                d1_out(a[0], a[1], a[2], eng)
            elif kind == "DM":
                d1_half(*a)
            else:
                d1_half_out(a[0], a[1], a[2], a[3], eng)
            if kind == "Q" and a == (1,):
                bias_cols()

        for name, eng in ORDER:
            run(name, eng)
